import numpy as np
import ml_dtypes


def mxq(x, axis, fmt="e4m3"):
    dtype, down = {"e4m3": (ml_dtypes.float8_e4m3fn, 7), "e5m2": (ml_dtypes.float8_e5m2, 14)}[fmt]
    v = np.moveaxis(np.asarray(x, np.float32).astype(ml_dtypes.bfloat16).astype(np.float64), axis, -1)
    blocks = v.reshape(v.shape[:-1] + (-1, 32))
    amax = np.abs(blocks).max(-1, keepdims=True)
    byte = np.maximum(np.where(amax > 0, np.frexp(amax)[1] - 1 + 127, 0) - down, 1)
    scale = np.exp2(byte - 127.0)
    codes = (blocks / scale).astype(np.float32).astype(dtype).astype(np.float64)
    return np.moveaxis((codes * scale).reshape(v.shape), -1, axis)


WIDE = False


def mx_kscale(k):
    if not WIDE:
        return np.ones(k)
    levels = np.array([20, -20, 10, -10, 0])
    a = np.random.permutation(np.resize(levels, k // 512 * 4)).reshape(k // 512, 4)
    idx = np.arange(k)
    return np.exp2(a[idx // 512, idx % 128 // 32])


BF16 = ml_dtypes.bfloat16


def bf(x):
    return np.asarray(x, np.float32).astype(BF16)


def f64(x):
    return np.asarray(x).astype(np.float64)


B, IN, OUT, R, Q, ORD = 16384, 1024, 1024, 8, 512, 3
K = R ** ORD


def setup_inputs():
    s = mx_kscale(Q)[:, None]
    z = np.random.standard_normal((ORD, R, B))
    g2 = np.random.standard_normal((Q, K)) / np.sqrt(K) / s
    g = np.random.standard_normal((Q, B)) * np.exp2(np.random.randint(-12, 1, (1, B))) * s
    return {"z": bf(z), "G2": bf(g2), "grad_out": bf(g)}


def reference(z, G2, grad_out):
    Z = f64(z)
    dk = mxq(f64(G2), 0, "e4m3").T @ mxq(f64(grad_out), 0, "e5m2")
    D = dk.reshape((R, R, R, B))
    t = (D * Z[2][:, None, None, :]).sum(axis=0)
    d0 = (t * Z[1][:, None, :]).sum(axis=0)
    d1 = (t * Z[0][None, :, :]).sum(axis=1)
    u = (D * Z[0][None, None, :, :]).sum(axis=2)
    d2 = (u * Z[1][None, :, :]).sum(axis=1)
    return np.stack([d0, d1, d2], axis=0)

@@ -1,0 +1,176 @@
+from contextlib import ExitStack
+
+import concourse.mybir as mybir
+from concourse.masks import make_identity
+
+F32 = mybir.dt.float32
+BF16 = mybir.dt.bfloat16
+U32 = mybir.dt.uint32
+U8 = mybir.dt.uint8
+E4M3_X4 = mybir.dt.float8_e4m3fn_x4
+E5M2_X4 = mybir.dt.float8_e5m2_x4
+MULT = mybir.AluOpType.mult
+ADD = mybir.AluOpType.add
+
+P = 128
+PACK = 4
+Q = P * PACK
+R = 8
+K = R * R * R
+B = 16384
+TILE = P
+LOAD_TILES = 8
+LOAD = LOAD_TILES * TILE
+GROUP_TILES = P // R
+GROUP = GROUP_TILES * TILE
+N_TILES = B // TILE
+
+FLOPS = 2 * Q * K * B
+
+
+def regroup(copy, grouped, raw):
+    copy(
+        out=grouped.rearrange("p (c i) j -> p c j i", i=4),
+        in_=raw.rearrange("p j (c i) -> p c j i", i=4),
+    )
+
+
+def accumulate(nc, acc, d_slice, weight, first):
+    if first:
+        nc.vector.tensor_scalar_mul(out=acc, in0=d_slice, scalar1=weight)
+    else:
+        nc.vector.scalar_tensor_tensor(
+            out=acc, in0=d_slice, scalar=weight, in1=acc, op0=MULT, op1=ADD
+        )
+
+
+def tile_fast_tucker_taylor_pa_t_kernel(tc, z, G2, grad_out, out):
+    nc = tc.nc
+    with ExitStack() as ctx:
+        keep = ctx.enter_context(tc.tile_pool(name="keep", bufs=1))
+        loads = ctx.enter_context(tc.tile_pool(name="loads", bufs=4))
+        stage = ctx.enter_context(tc.tile_pool(name="stage", bufs=2))
+        operand = ctx.enter_context(tc.tile_pool(name="operand", bufs=3))
+        partial = ctx.enter_context(tc.tile_pool(name="partial", bufs=2))
+        products = ctx.enter_context(tc.tile_pool(name="products", bufs=3))
+        banks = ctx.enter_context(tc.psum_pool(name="banks", bufs=6))
+        sums_pool = ctx.enter_context(tc.psum_pool(name="sums", bufs=2))
+
+        ident_bf = keep.tile([P, P], BF16)
+        make_identity(nc, ident_bf[:])
+        ident = keep.tile([P, P], F32)
+        make_identity(nc, ident[:])
+
+        g2_raw = keep.tile([P, PACK, K], BF16)
+        nc.sync.dma_start(out=g2_raw[:], in_=G2.rearrange("(p j) k -> p j k", j=PACK))
+        g2_grouped = keep.tile([P, K, PACK], BF16, align_bytes=64)
+        regroup(nc.vector.tensor_copy, g2_grouped[:], g2_raw[:])
+        g2_codes = keep.tile([P, K], U32, align_bytes=64)
+        g2_scales = keep.tile([P, K], U8, align_bytes=64)
+        nc.vector.quantize_mx(
+            out=g2_codes[:].bitcast(E4M3_X4),
+            scales=g2_scales[:],
+            in_=g2_grouped[:].rearrange("p k j -> p (k j)"),
+        )
+
+        z_rows = keep.tile([P, 3, B // GROUP_TILES], BF16)
+        nc.sync.dma_start(out=z_rows[:], in_=z.rearrange("i r (t x) -> (r t) i x", t=GROUP_TILES))
+        z_t = keep.tile([P, N_TILES, 3, R], F32)
+        for i in range(3):
+            z_bank = banks.tile([P, R, TILE], BF16, tag="bank", name="z_bank")
+            for g in range(R):
+                nc.tensor.transpose(
+                    z_bank[:, g, :], z_rows[:, i, g * TILE : (g + 1) * TILE], ident_bf[:]
+                )
+            nc.vector.tensor_copy(
+                out=z_t[:, :, i, :].rearrange("p (t g) r -> p g t r", g=R),
+                in_=z_bank[:].rearrange("p g (r t) -> p g t r", t=GROUP_TILES),
+            )
+
+        g_rows = grad_out.rearrange("(p j) n -> p j n", j=PACK)
+
+        for group in range(B // GROUP):
+            first_tile = group * GROUP_TILES
+            t_part = partial.tile([P, GROUP_TILES, R, R], F32)
+            u_part = partial.tile([P, GROUP_TILES, R, R], F32)
+
+            for load in range(GROUP_TILES // LOAD_TILES):
+                start = group * GROUP + load * LOAD
+                raw = loads.tile([P, PACK, LOAD], BF16)
+                nc.sync.dma_start(out=raw[:], in_=g_rows[:, :, start : start + LOAD])
+                grouped = stage.tile([P, LOAD, PACK], BF16, align_bytes=64)
+                regroup(nc.scalar.copy, grouped[:], raw[:])
+                codes = operand.tile([P, LOAD], U32, align_bytes=64)
+                scales = operand.tile([P, LOAD], U8, align_bytes=64)
+                nc.vector.quantize_mx(
+                    out=codes[:].bitcast(E5M2_X4),
+                    scales=scales[:],
+                    in_=grouped[:].rearrange("p w j -> p (w j)"),
+                )
+
+                for pair in range(LOAD_TILES // 2):
+                    pair_banks = []
+                    for s in range(2):
+                        local = pair * 2 + s
+                        cols = slice(local * TILE, (local + 1) * TILE)
+                        d_bank = banks.tile([P, K], F32, tag="bank", name="d_bank")
+                        nc.tensor.matmul_mx(
+                            out=d_bank[:],
+                            lhsT=codes[:, cols].bitcast(E5M2_X4),
+                            lhsT_scale=scales[:, cols],
+                            rhs=g2_codes[:].bitcast(E4M3_X4),
+                            rhs_scale=g2_scales[:],
+                            start=True,
+                            stop=True,
+                        )
+                        pair_banks.append((load * LOAD_TILES + local, d_bank))
+                    for step in range(R):
+                        for k, d_bank in pair_banks:
+                            accumulate(
+                                nc,
+                                t_part[:, k].rearrange("p b a -> p (b a)"),
+                                d_bank[:, step * R * R : (step + 1) * R * R],
+                                z_t[:, first_tile + k, 2, step : step + 1],
+                                step == 0,
+                            )
+                            accumulate(
+                                nc,
+                                u_part[:, k].rearrange("p c b -> p (c b)"),
+                                d_bank[:].rearrange("p (cb a) -> p cb a", a=R)[:, :, step],
+                                z_t[:, first_tile + k, 0, step : step + 1],
+                                step == 0,
+                            )
+
+            tiles = slice(first_tile, first_tile + GROUP_TILES)
+            sums = sums_pool.tile([P, 3, TILE], F32)
+            second = (
+                (t_part[:], 1),
+                (u_part[:], 2),
+                (u_part[:].rearrange("p t c b -> p t b c"), 1),
+            )
+            for i, (part, factor) in enumerate(second):
+                prod = products.tile([P, R, GROUP_TILES, R], F32)
+                nc.vector.tensor_tensor(
+                    out=prod[:].rearrange("p k t r -> p t k r"),
+                    in0=part,
+                    in1=z_t[:, tiles, factor, :].unsqueeze(3).to_broadcast([P, GROUP_TILES, R, R]),
+                    op=MULT,
+                )
+                for k in range(R):
+                    nc.tensor.matmul(
+                        out=sums[:, i, :],
+                        lhsT=prod[:, k].rearrange("p t r -> p (t r)"),
+                        rhs=ident[:],
+                        is_transpose=True,
+                        start=(k == 0),
+                        stop=(k == R - 1),
+                    )
+            result = products.tile([P, 3, TILE], F32)
+            nc.scalar.copy(out=result[:], in_=sums[:])
+            for r in range(R):
+                nc.sync.dma_start(
+                    out=out[:, r, group * GROUP : (group + 1) * GROUP].rearrange(
+                        "i (t m) -> t i m", m=TILE
+                    ),
+                    in_=result[r:P:R, :, :],
+                )

@@ -11,19 +11,24 @@ E4M3_X4 = mybir.dt.float8_e4m3fn_x4
 E5M2_X4 = mybir.dt.float8_e5m2_x4
 MULT = mybir.AluOpType.mult
 ADD = mybir.AluOpType.add
+COPY = mybir.ActivationFunctionType.Copy
 
 P = 128
 PACK = 4
 Q = P * PACK
 R = 8
+RR = R * R
 K = R * R * R
 B = 16384
 TILE = P
+N_TILES = B // TILE
 LOAD_TILES = 8
 LOAD = LOAD_TILES * TILE
+N_LOADS = B // LOAD
 GROUP_TILES = P // R
 GROUP = GROUP_TILES * TILE
-N_TILES = B // TILE
+QUAD = 4
+VECTOR_REGROUPS = 5
 
 FLOPS = 2 * Q * K * B
 
@@ -33,6 +38,14 @@ def regroup(copy, grouped, raw):
         out=grouped.rearrange("p (c i) j -> p c j i", i=4),
         in_=raw.rearrange("p j (c i) -> p c j i", i=4),
     )
+
+
+def slice_c(d_bank, c):
+    return d_bank[:, c * RR : (c + 1) * RR]
+
+
+def slice_a(d_bank, a):
+    return d_bank[:].rearrange("p (cb a) -> p cb a", a=R)[:, :, a]
 
 
 def accumulate(nc, acc, d_slice, weight, first):
@@ -48,13 +61,15 @@ def tile_fast_tucker_taylor_pa_t_kernel(tc, z, G2, grad_out, out):
     nc = tc.nc
     with ExitStack() as ctx:
         keep = ctx.enter_context(tc.tile_pool(name="keep", bufs=1))
-        loads = ctx.enter_context(tc.tile_pool(name="loads", bufs=4))
+        loads = ctx.enter_context(tc.tile_pool(name="loads", bufs=3))
         stage = ctx.enter_context(tc.tile_pool(name="stage", bufs=2))
         operand = ctx.enter_context(tc.tile_pool(name="operand", bufs=3))
         partial = ctx.enter_context(tc.tile_pool(name="partial", bufs=2))
+        weighted = ctx.enter_context(tc.tile_pool(name="weighted", bufs=2))
         products = ctx.enter_context(tc.tile_pool(name="products", bufs=3))
-        banks = ctx.enter_context(tc.psum_pool(name="banks", bufs=6))
-        sums_pool = ctx.enter_context(tc.psum_pool(name="sums", bufs=2))
+        vector_banks = ctx.enter_context(tc.psum_pool(name="vector_banks", bufs=4))
+        scalar_banks = ctx.enter_context(tc.psum_pool(name="scalar_banks", bufs=2))
+        turn_banks = ctx.enter_context(tc.psum_pool(name="turn_banks", bufs=2))
 
         ident_bf = keep.tile([P, P], BF16)
         make_identity(nc, ident_bf[:])
@@ -73,11 +88,45 @@ def tile_fast_tucker_taylor_pa_t_kernel(tc, z, G2, grad_out, out):
             in_=g2_grouped[:].rearrange("p k j -> p (k j)"),
         )
 
+        g_rows = grad_out.rearrange("(p j) n -> p j n", j=PACK)
+
+        def prepare(load):
+            raw = loads.tile([P, PACK, LOAD], BF16, name="raw")
+            nc.sync.dma_start(out=raw[:], in_=g_rows[:, :, load * LOAD : (load + 1) * LOAD])
+            grouped = stage.tile([P, LOAD, PACK], BF16, align_bytes=64, name="grouped")
+            cut = VECTOR_REGROUPS * TILE
+            regroup(nc.vector.tensor_copy, grouped[:, :cut, :], raw[:, :, :cut])
+            regroup(nc.scalar.copy, grouped[:, cut:, :], raw[:, :, cut:])
+            codes = operand.tile([P, LOAD], U32, align_bytes=64, name="codes")
+            scales = operand.tile([P, LOAD], U8, align_bytes=64, name="scales")
+            nc.vector.quantize_mx(
+                out=codes[:].bitcast(E5M2_X4),
+                scales=scales[:],
+                in_=grouped[:].rearrange("p w j -> p (w j)"),
+            )
+            return codes, scales
+
+        def d_of_tile(pool, codes, scales, local):
+            cols = slice(local * TILE, (local + 1) * TILE)
+            d_bank = pool.tile([P, K], F32, tag="bank", name="d_bank")
+            nc.tensor.matmul_mx(
+                out=d_bank[:],
+                lhsT=codes[:, cols].bitcast(E5M2_X4),
+                lhsT_scale=scales[:, cols],
+                rhs=g2_codes[:].bitcast(E4M3_X4),
+                rhs_scale=g2_scales[:],
+                start=True,
+                stop=True,
+            )
+            return d_bank
+
+        ready = prepare(0)
+
         z_rows = keep.tile([P, 3, B // GROUP_TILES], BF16)
         nc.sync.dma_start(out=z_rows[:], in_=z.rearrange("i r (t x) -> (r t) i x", t=GROUP_TILES))
         z_t = keep.tile([P, N_TILES, 3, R], F32)
         for i in range(3):
-            z_bank = banks.tile([P, R, TILE], BF16, tag="bank", name="z_bank")
+            z_bank = vector_banks.tile([P, R, TILE], BF16, tag="bank", name="z_bank")
             for g in range(R):
                 nc.tensor.transpose(
                     z_bank[:, g, :], z_rows[:, i, g * TILE : (g + 1) * TILE], ident_bf[:]
@@ -87,72 +136,87 @@ def tile_fast_tucker_taylor_pa_t_kernel(tc, z, G2, grad_out, out):
                 in_=z_bank[:].rearrange("p g (r t) -> p g t r", t=GROUP_TILES),
             )
 
-        g_rows = grad_out.rearrange("(p j) n -> p j n", j=PACK)
+        part = None
+        for load in range(N_LOADS):
+            codes, scales = ready
+            if load + 1 < N_LOADS:
+                ready = prepare(load + 1)
+            load_tile = load * LOAD_TILES
+            group = load_tile // GROUP_TILES
+            group_tile = group * GROUP_TILES
+            if load_tile == group_tile:
+                part = partial.tile([P, 2, GROUP_TILES, RR], F32, name="part")
 
-        for group in range(B // GROUP):
-            first_tile = group * GROUP_TILES
-            t_part = partial.tile([P, GROUP_TILES, R, R], F32)
-            u_part = partial.tile([P, GROUP_TILES, R, R], F32)
+            for quad in range(LOAD_TILES // QUAD):
+                local = quad * QUAD
 
-            for load in range(GROUP_TILES // LOAD_TILES):
-                start = group * GROUP + load * LOAD
-                raw = loads.tile([P, PACK, LOAD], BF16)
-                nc.sync.dma_start(out=raw[:], in_=g_rows[:, :, start : start + LOAD])
-                grouped = stage.tile([P, LOAD, PACK], BF16, align_bytes=64)
-                regroup(nc.scalar.copy, grouped[:], raw[:])
-                codes = operand.tile([P, LOAD], U32, align_bytes=64)
-                scales = operand.tile([P, LOAD], U8, align_bytes=64)
-                nc.vector.quantize_mx(
-                    out=codes[:].bitcast(E5M2_X4),
-                    scales=scales[:],
-                    in_=grouped[:].rearrange("p w j -> p (w j)"),
+                pair = [(local + s, d_of_tile(vector_banks, codes, scales, local + s)) for s in range(2)]
+                for step in range(R):
+                    for number, d_bank in pair:
+                        tile_no = load_tile + number
+                        k = tile_no - group_tile
+                        accumulate(
+                            nc, part[:, 0, k, :], slice_c(d_bank, step),
+                            z_t[:, tile_no, 2, step : step + 1], step == 0,
+                        )
+                        accumulate(
+                            nc, part[:, 1, k, :], slice_a(d_bank, step),
+                            z_t[:, tile_no, 0, step : step + 1], step == 0,
+                        )
+
+                t_terms = weighted.tile([P, R, 2, RR], F32, name="t_terms")
+                u_terms = weighted.tile([P, R, 2, RR], F32, name="u_terms")
+                for s in range(2):
+                    tile_no = load_tile + local + 2 + s
+                    d_bank = d_of_tile(scalar_banks, codes, scales, local + 2 + s)
+                    for step in range(R):
+                        nc.scalar.activation(
+                            out=t_terms[:, step, s, :], in_=slice_c(d_bank, step), func=COPY,
+                            scale=z_t[:, tile_no, 2, step : step + 1],
+                        )
+                    for step in range(R):
+                        nc.scalar.activation(
+                            out=u_terms[:, step, s, :], in_=slice_a(d_bank, step), func=COPY,
+                            scale=z_t[:, tile_no, 0, step : step + 1],
+                        )
+                turned = turn_banks.tile([P, 2, TILE], F32, tag="turn", name="turned")
+                for which, terms in enumerate((t_terms, u_terms)):
+                    for step in range(R):
+                        nc.tensor.matmul(
+                            out=turned[:, which, :],
+                            lhsT=terms[:, step].rearrange("p s x -> p (s x)"),
+                            rhs=ident[:],
+                            is_transpose=True,
+                            start=(step == 0),
+                            stop=(step == R - 1),
+                        )
+                turned_sb = weighted.tile([P, 2, TILE], F32, name="turned_sb")
+                nc.scalar.copy(out=turned_sb[:], in_=turned[:])
+                back = turn_banks.tile([P, 2, TILE], F32, tag="turn", name="back")
+                for which in range(2):
+                    nc.tensor.transpose(back[:, which, :], turned_sb[:, which, :], ident[:])
+                k = load_tile + local + 2 - group_tile
+                nc.scalar.copy(
+                    out=part[:, :, k : k + 2, :].rearrange("p w s x -> p w (s x)"), in_=back[:]
                 )
 
-                for pair in range(LOAD_TILES // 2):
-                    pair_banks = []
-                    for s in range(2):
-                        local = pair * 2 + s
-                        cols = slice(local * TILE, (local + 1) * TILE)
-                        d_bank = banks.tile([P, K], F32, tag="bank", name="d_bank")
-                        nc.tensor.matmul_mx(
-                            out=d_bank[:],
-                            lhsT=codes[:, cols].bitcast(E5M2_X4),
-                            lhsT_scale=scales[:, cols],
-                            rhs=g2_codes[:].bitcast(E4M3_X4),
-                            rhs_scale=g2_scales[:],
-                            start=True,
-                            stop=True,
-                        )
-                        pair_banks.append((load * LOAD_TILES + local, d_bank))
-                    for step in range(R):
-                        for k, d_bank in pair_banks:
-                            accumulate(
-                                nc,
-                                t_part[:, k].rearrange("p b a -> p (b a)"),
-                                d_bank[:, step * R * R : (step + 1) * R * R],
-                                z_t[:, first_tile + k, 2, step : step + 1],
-                                step == 0,
-                            )
-                            accumulate(
-                                nc,
-                                u_part[:, k].rearrange("p c b -> p (c b)"),
-                                d_bank[:].rearrange("p (cb a) -> p cb a", a=R)[:, :, step],
-                                z_t[:, first_tile + k, 0, step : step + 1],
-                                step == 0,
-                            )
+            if load_tile + LOAD_TILES < group_tile + GROUP_TILES:
+                continue
 
-            tiles = slice(first_tile, first_tile + GROUP_TILES)
-            sums = sums_pool.tile([P, 3, TILE], F32)
+            tiles = slice(group_tile, group_tile + GROUP_TILES)
+            t_part = part[:, 0].rearrange("p t (b a) -> p t b a", a=R)
+            u_part = part[:, 1].rearrange("p t (c b) -> p t c b", b=R)
             second = (
-                (t_part[:], 1),
-                (u_part[:], 2),
-                (u_part[:].rearrange("p t c b -> p t b c"), 1),
+                (t_part, 1),
+                (u_part, 2),
+                (u_part.rearrange("p t c b -> p t b c"), 1),
             )
-            for i, (part, factor) in enumerate(second):
-                prod = products.tile([P, R, GROUP_TILES, R], F32)
+            sums = turn_banks.tile([P, 3, TILE], F32, tag="turn", name="sums")
+            for i, (first_sum, factor) in enumerate(second):
+                prod = products.tile([P, R, GROUP_TILES, R], F32, name="prod")
                 nc.vector.tensor_tensor(
                     out=prod[:].rearrange("p k t r -> p t k r"),
-                    in0=part,
+                    in0=first_sum,
                     in1=z_t[:, tiles, factor, :].unsqueeze(3).to_broadcast([P, GROUP_TILES, R, R]),
                     op=MULT,
                 )
@@ -165,7 +229,7 @@ def tile_fast_tucker_taylor_pa_t_kernel(tc, z, G2, grad_out, out):
                         start=(k == 0),
                         stop=(k == R - 1),
                     )
-            result = products.tile([P, 3, TILE], F32)
+            result = products.tile([P, 3, TILE], F32, name="result")
             nc.scalar.copy(out=result[:], in_=sums[:])
             for r in range(R):
                 nc.sync.dma_start(

@@ -22,13 +22,14 @@ K = R * R * R
 B = 16384
 TILE = P
 N_TILES = B // TILE
-LOAD_TILES = 8
-LOAD = LOAD_TILES * TILE
-N_LOADS = B // LOAD
 GROUP_TILES = P // R
 GROUP = GROUP_TILES * TILE
 QUAD = 4
-VECTOR_REGROUPS = 5
+LOAD = QUAD * TILE
+N_QUADS = B // LOAD
+GROUP_QUADS = GROUP_TILES // QUAD
+VECTOR_REGROUPS = 256
+LOADS_AHEAD = 4
 
 FLOPS = 2 * Q * K * B
 
@@ -61,180 +62,237 @@ def tile_fast_tucker_taylor_pa_t_kernel(tc, z, G2, grad_out, out):
     nc = tc.nc
     with ExitStack() as ctx:
         keep = ctx.enter_context(tc.tile_pool(name="keep", bufs=1))
-        loads = ctx.enter_context(tc.tile_pool(name="loads", bufs=3))
+        loads = ctx.enter_context(tc.tile_pool(name="loads", bufs=LOADS_AHEAD))
         stage = ctx.enter_context(tc.tile_pool(name="stage", bufs=2))
         operand = ctx.enter_context(tc.tile_pool(name="operand", bufs=3))
         partial = ctx.enter_context(tc.tile_pool(name="partial", bufs=2))
         weighted = ctx.enter_context(tc.tile_pool(name="weighted", bufs=2))
-        products = ctx.enter_context(tc.tile_pool(name="products", bufs=3))
+        products = ctx.enter_context(tc.tile_pool(name="products", bufs=2))
         vector_banks = ctx.enter_context(tc.psum_pool(name="vector_banks", bufs=4))
         scalar_banks = ctx.enter_context(tc.psum_pool(name="scalar_banks", bufs=2))
-        turn_banks = ctx.enter_context(tc.psum_pool(name="turn_banks", bufs=2))
-
-        ident_bf = keep.tile([P, P], BF16)
-        make_identity(nc, ident_bf[:])
-        ident = keep.tile([P, P], F32)
-        make_identity(nc, ident[:])
-
-        g2_raw = keep.tile([P, PACK, K], BF16)
-        nc.sync.dma_start(out=g2_raw[:], in_=G2.rearrange("(p j) k -> p j k", j=PACK))
-        g2_grouped = keep.tile([P, K, PACK], BF16, align_bytes=64)
-        regroup(nc.vector.tensor_copy, g2_grouped[:], g2_raw[:])
-        g2_codes = keep.tile([P, K], U32, align_bytes=64)
-        g2_scales = keep.tile([P, K], U8, align_bytes=64)
-        nc.vector.quantize_mx(
-            out=g2_codes[:].bitcast(E4M3_X4),
-            scales=g2_scales[:],
-            in_=g2_grouped[:].rearrange("p k j -> p (k j)"),
-        )
+        turn_bank = ctx.enter_context(tc.psum_pool(name="turn_bank", bufs=1))
+        sums_bank = ctx.enter_context(tc.psum_pool(name="sums_bank", bufs=1))
+        ctx.enter_context(tc.manual_schedule())
 
         g_rows = grad_out.rearrange("(p j) n -> p j n", j=PACK)
+        g2_codes = keep.tile([P, K], U32, align_bytes=64)
+        g2_scales = keep.tile([P, K], U8, align_bytes=64)
+        z_t = keep.tile([P, N_TILES, 3, R], F32)
+        ident = keep.tile([P, P], F32)
 
-        def prepare(load):
-            raw = loads.tile([P, PACK, LOAD], BF16, name="raw")
-            nc.sync.dma_start(out=raw[:], in_=g_rows[:, :, load * LOAD : (load + 1) * LOAD])
-            grouped = stage.tile([P, LOAD, PACK], BF16, align_bytes=64, name="grouped")
-            cut = VECTOR_REGROUPS * TILE
-            regroup(nc.vector.tensor_copy, grouped[:, :cut, :], raw[:, :, :cut])
-            regroup(nc.scalar.copy, grouped[:, cut:, :], raw[:, :, cut:])
-            codes = operand.tile([P, LOAD], U32, align_bytes=64, name="codes")
-            scales = operand.tile([P, LOAD], U8, align_bytes=64, name="scales")
+        raw, grouped, codes, scales = {}, {}, {}, {}
+        d_banks, terms, turned, turned_sb, back = {}, {}, {}, {}, {}
+        part, prod, sums, result = {}, {}, {}, {}
+
+        def load(q):
+            raw[q] = loads.tile([P, PACK, LOAD], BF16, name="raw")
+            nc.sync.dma_start(out=raw[q][:], in_=g_rows[:, :, q * LOAD : (q + 1) * LOAD])
+
+        def regroup_on_vector(q):
+            grouped[q] = stage.tile([P, LOAD, PACK], BF16, align_bytes=64, name="grouped")
+            cut = VECTOR_REGROUPS
+            regroup(nc.vector.tensor_copy, grouped[q][:, :cut, :], raw[q][:, :, :cut])
+
+        def regroup_on_scalar(q):
+            cut = VECTOR_REGROUPS
+            regroup(nc.scalar.copy, grouped[q][:, cut:, :], raw[q][:, :, cut:])
+
+        def quantise(q):
+            codes[q] = operand.tile([P, LOAD], U32, align_bytes=64, name="codes")
+            scales[q] = operand.tile([P, LOAD], U8, align_bytes=64, name="scales")
             nc.vector.quantize_mx(
-                out=codes[:].bitcast(E5M2_X4),
-                scales=scales[:],
-                in_=grouped[:].rearrange("p w j -> p (w j)"),
+                out=codes[q][:].bitcast(E5M2_X4),
+                scales=scales[q][:],
+                in_=grouped[q][:].rearrange("p w j -> p (w j)"),
             )
-            return codes, scales
 
-        def d_of_tile(pool, codes, scales, local):
-            cols = slice(local * TILE, (local + 1) * TILE)
-            d_bank = pool.tile([P, K], F32, tag="bank", name="d_bank")
+        def multiply(q, s, pool):
+            cols = slice(s * TILE, (s + 1) * TILE)
+            d_banks[q, s] = pool.tile([P, K], F32, tag="bank", name="d_bank")
             nc.tensor.matmul_mx(
-                out=d_bank[:],
-                lhsT=codes[:, cols].bitcast(E5M2_X4),
-                lhsT_scale=scales[:, cols],
+                out=d_banks[q, s][:],
+                lhsT=codes[q][:, cols].bitcast(E5M2_X4),
+                lhsT_scale=scales[q][:, cols],
                 rhs=g2_codes[:].bitcast(E4M3_X4),
                 rhs_scale=g2_scales[:],
                 start=True,
                 stop=True,
             )
-            return d_bank
 
-        ready = prepare(0)
+        def part_of(q):
+            g = q // GROUP_QUADS
+            if g not in part:
+                part[g] = partial.tile([P, 2, GROUP_TILES, RR], F32, name="part")
+            return part[g], (q % GROUP_QUADS) * QUAD
 
+        def chains(q):
+            group_part, k = part_of(q)
+            for step in range(R):
+                for s in range(2):
+                    tile_no = q * QUAD + s
+                    accumulate(
+                        nc, group_part[:, 0, k + s, :], slice_c(d_banks[q, s], step),
+                        z_t[:, tile_no, 2, step : step + 1], step == 0,
+                    )
+                    accumulate(
+                        nc, group_part[:, 1, k + s, :], slice_a(d_banks[q, s], step),
+                        z_t[:, tile_no, 0, step : step + 1], step == 0,
+                    )
+
+        def weigh(q, s):
+            if s == 0:
+                terms[q] = (
+                    weighted.tile([P, R, 2, RR], F32, name="t_terms"),
+                    weighted.tile([P, R, 2, RR], F32, name="u_terms"),
+                )
+            t_terms, u_terms = terms[q]
+            tile_no = q * QUAD + 2 + s
+            d_bank = d_banks[q, 2 + s]
+            for step in range(R):
+                nc.scalar.activation(
+                    out=t_terms[:, step, s, :], in_=slice_c(d_bank, step), func=COPY,
+                    scale=z_t[:, tile_no, 2, step : step + 1],
+                )
+            for step in range(R):
+                nc.scalar.activation(
+                    out=u_terms[:, step, s, :], in_=slice_a(d_bank, step), func=COPY,
+                    scale=z_t[:, tile_no, 0, step : step + 1],
+                )
+
+        def add_up(bank_cols, slabs):
+            for step in range(R):
+                nc.tensor.matmul(
+                    out=bank_cols, lhsT=slabs[:, step].rearrange("p s x -> p (s x)"), rhs=ident[:],
+                    is_transpose=True, start=(step == 0), stop=(step == R - 1),
+                )
+
+        def add_terms(q):
+            turned[q] = turn_bank.tile([P, 2, TILE], F32, tag="turn", name="turned")
+            for which in range(2):
+                add_up(turned[q][:, which, :], terms[q][which])
+
+        def copy_turned(q):
+            turned_sb[q] = weighted.tile([P, 2, TILE], F32, name="turned_sb")
+            nc.scalar.copy(out=turned_sb[q][:], in_=turned[q][:])
+
+        def turn_back(q):
+            back[q] = turn_bank.tile([P, 2, TILE], F32, tag="turn", name="back")
+            for which in range(2):
+                nc.tensor.transpose(back[q][:, which, :], turned_sb[q][:, which, :], ident[:])
+
+        def copy_back(q):
+            group_part, k = part_of(q)
+            nc.scalar.copy(
+                out=group_part[:, :, k + 2 : k + 4, :].rearrange("p w s x -> p w (s x)"),
+                in_=back[q][:],
+            )
+
+        def second_product(g, i):
+            tiles = slice(g * GROUP_TILES, (g + 1) * GROUP_TILES)
+            t_part = part[g][:, 0].rearrange("p t (b a) -> p t b a", a=R)
+            u_part = part[g][:, 1].rearrange("p t (c b) -> p t c b", b=R)
+            first_sum, factor = (
+                (t_part, 1),
+                (u_part, 2),
+                (u_part.rearrange("p t c b -> p t b c"), 1),
+            )[i]
+            prod[g, i] = products.tile([P, R, GROUP_TILES, R], F32, name="prod")
+            nc.vector.tensor_tensor(
+                out=prod[g, i][:].rearrange("p k t r -> p t k r"),
+                in0=first_sum,
+                in1=z_t[:, tiles, factor, :].unsqueeze(3).to_broadcast([P, GROUP_TILES, R, R]),
+                op=MULT,
+            )
+
+        def second_sum(g, i):
+            if i == 0:
+                sums[g] = sums_bank.tile([P, 3, TILE], F32, name="sums")
+            add_up(sums[g][:, i, :], prod[g, i])
+
+        def copy_result(g):
+            result[g] = products.tile([P, 3, TILE], F32, name="result")
+            nc.scalar.copy(out=result[g][:], in_=sums[g][:])
+
+        def store(g):
+            for r in range(R):
+                nc.sync.dma_start(
+                    out=out[:, r, g * GROUP : (g + 1) * GROUP].rearrange("i (t m) -> t i m", m=TILE),
+                    in_=result[g][r:P:R, :, :],
+                )
+
+        g2_raw = keep.tile([P, PACK, K], BF16)
+        nc.sync.dma_start(out=g2_raw[:], in_=G2.rearrange("(p j) k -> p j k", j=PACK))
+        load(0)
         z_rows = keep.tile([P, 3, B // GROUP_TILES], BF16)
         nc.sync.dma_start(out=z_rows[:], in_=z.rearrange("i r (t x) -> (r t) i x", t=GROUP_TILES))
-        z_t = keep.tile([P, N_TILES, 3, R], F32)
+        for q in range(1, LOADS_AHEAD):
+            load(q)
+        ident_bf = keep.tile([P, P], BF16)
+        make_identity(nc, ident_bf[:])
+        make_identity(nc, ident[:])
+
+        g2_grouped = keep.tile([P, K, PACK], BF16, align_bytes=64)
+        regroup(nc.vector.tensor_copy, g2_grouped[:], g2_raw[:])
+        regroup_on_vector(0)
+        regroup_on_scalar(0)
+        nc.vector.quantize_mx(
+            out=g2_codes[:].bitcast(E4M3_X4),
+            scales=g2_scales[:],
+            in_=g2_grouped[:].rearrange("p k j -> p (k j)"),
+        )
         for i in range(3):
             z_bank = vector_banks.tile([P, R, TILE], BF16, tag="bank", name="z_bank")
             for g in range(R):
                 nc.tensor.transpose(
                     z_bank[:, g, :], z_rows[:, i, g * TILE : (g + 1) * TILE], ident_bf[:]
                 )
-            nc.vector.tensor_copy(
+            nc.scalar.copy(
                 out=z_t[:, :, i, :].rearrange("p (t g) r -> p g t r", g=R),
                 in_=z_bank[:].rearrange("p g (r t) -> p g t r", t=GROUP_TILES),
             )
+        regroup_on_vector(1)
+        regroup_on_scalar(1)
+        quantise(0)
+        multiply(0, 0, vector_banks)
+        multiply(0, 1, vector_banks)
+        multiply(0, 2, scalar_banks)
 
-        part = None
-        for load in range(N_LOADS):
-            codes, scales = ready
-            if load + 1 < N_LOADS:
-                ready = prepare(load + 1)
-            load_tile = load * LOAD_TILES
-            group = load_tile // GROUP_TILES
-            group_tile = group * GROUP_TILES
-            if load_tile == group_tile:
-                part = partial.tile([P, 2, GROUP_TILES, RR], F32, name="part")
+        def quad(q):
+            return 0 <= q < N_QUADS
 
-            for quad in range(LOAD_TILES // QUAD):
-                local = quad * QUAD
-
-                pair = [(local + s, d_of_tile(vector_banks, codes, scales, local + s)) for s in range(2)]
-                for step in range(R):
-                    for number, d_bank in pair:
-                        tile_no = load_tile + number
-                        k = tile_no - group_tile
-                        accumulate(
-                            nc, part[:, 0, k, :], slice_c(d_bank, step),
-                            z_t[:, tile_no, 2, step : step + 1], step == 0,
-                        )
-                        accumulate(
-                            nc, part[:, 1, k, :], slice_a(d_bank, step),
-                            z_t[:, tile_no, 0, step : step + 1], step == 0,
-                        )
-
-                t_terms = weighted.tile([P, R, 2, RR], F32, name="t_terms")
-                u_terms = weighted.tile([P, R, 2, RR], F32, name="u_terms")
-                for s in range(2):
-                    tile_no = load_tile + local + 2 + s
-                    d_bank = d_of_tile(scalar_banks, codes, scales, local + 2 + s)
-                    for step in range(R):
-                        nc.scalar.activation(
-                            out=t_terms[:, step, s, :], in_=slice_c(d_bank, step), func=COPY,
-                            scale=z_t[:, tile_no, 2, step : step + 1],
-                        )
-                    for step in range(R):
-                        nc.scalar.activation(
-                            out=u_terms[:, step, s, :], in_=slice_a(d_bank, step), func=COPY,
-                            scale=z_t[:, tile_no, 0, step : step + 1],
-                        )
-                turned = turn_banks.tile([P, 2, TILE], F32, tag="turn", name="turned")
-                for which, terms in enumerate((t_terms, u_terms)):
-                    for step in range(R):
-                        nc.tensor.matmul(
-                            out=turned[:, which, :],
-                            lhsT=terms[:, step].rearrange("p s x -> p (s x)"),
-                            rhs=ident[:],
-                            is_transpose=True,
-                            start=(step == 0),
-                            stop=(step == R - 1),
-                        )
-                turned_sb = weighted.tile([P, 2, TILE], F32, name="turned_sb")
-                nc.scalar.copy(out=turned_sb[:], in_=turned[:])
-                back = turn_banks.tile([P, 2, TILE], F32, tag="turn", name="back")
-                for which in range(2):
-                    nc.tensor.transpose(back[:, which, :], turned_sb[:, which, :], ident[:])
-                k = load_tile + local + 2 - group_tile
-                nc.scalar.copy(
-                    out=part[:, :, k : k + 2, :].rearrange("p w s x -> p w (s x)"), in_=back[:]
-                )
-
-            if load_tile + LOAD_TILES < group_tile + GROUP_TILES:
-                continue
-
-            tiles = slice(group_tile, group_tile + GROUP_TILES)
-            t_part = part[:, 0].rearrange("p t (b a) -> p t b a", a=R)
-            u_part = part[:, 1].rearrange("p t (c b) -> p t c b", b=R)
-            second = (
-                (t_part, 1),
-                (u_part, 2),
-                (u_part.rearrange("p t c b -> p t b c"), 1),
-            )
-            sums = turn_banks.tile([P, 3, TILE], F32, tag="turn", name="sums")
-            for i, (first_sum, factor) in enumerate(second):
-                prod = products.tile([P, R, GROUP_TILES, R], F32, name="prod")
-                nc.vector.tensor_tensor(
-                    out=prod[:].rearrange("p k t r -> p t k r"),
-                    in0=first_sum,
-                    in1=z_t[:, tiles, factor, :].unsqueeze(3).to_broadcast([P, GROUP_TILES, R, R]),
-                    op=MULT,
-                )
-                for k in range(R):
-                    nc.tensor.matmul(
-                        out=sums[:, i, :],
-                        lhsT=prod[:, k].rearrange("p t r -> p (t r)"),
-                        rhs=ident[:],
-                        is_transpose=True,
-                        start=(k == 0),
-                        stop=(k == R - 1),
-                    )
-            result = products.tile([P, 3, TILE], F32, name="result")
-            nc.scalar.copy(out=result[:], in_=sums[:])
-            for r in range(R):
-                nc.sync.dma_start(
-                    out=out[:, r, group * GROUP : (group + 1) * GROUP].rearrange(
-                        "i (t m) -> t i m", m=TILE
-                    ),
-                    in_=result[r:P:R, :, :],
-                )
+        for q in range(N_QUADS + GROUP_QUADS + 1):
+            g, i = divmod(q - GROUP_QUADS - 1, GROUP_QUADS)
+            if quad(q + LOADS_AHEAD):
+                load(q + LOADS_AHEAD)
+            if g >= 0 and i == 3:
+                store(g)
+            if quad(q + 1):
+                quantise(q + 1)
+            if quad(q - 1):
+                add_terms(q - 1)
+            if quad(q):
+                multiply(q, 3, scalar_banks)
+            if quad(q + 1):
+                multiply(q + 1, 0, vector_banks)
+                multiply(q + 1, 1, vector_banks)
+            if quad(q):
+                weigh(q, 0)
+            if quad(q + 1):
+                multiply(q + 1, 2, scalar_banks)
+            if quad(q - 1):
+                copy_turned(q - 1)
+                turn_back(q - 1)
+            if quad(q):
+                weigh(q, 1)
+            if quad(q - 1):
+                copy_back(q - 1)
+            if g >= 0 and i < 3:
+                second_product(g, i)
+                second_sum(g, i)
+            if quad(q + 2):
+                regroup_on_vector(q + 2)
+                regroup_on_scalar(q + 2)
+            if quad(q):
+                chains(q)
+            if g >= 0 and i == 2:
+                copy_result(g)

@@ -28,7 +28,6 @@ QUAD = 4
 LOAD = QUAD * TILE
 N_QUADS = B // LOAD
 GROUP_QUADS = GROUP_TILES // QUAD
-VECTOR_REGROUPS = 256
 LOADS_AHEAD = 4
 
 FLOPS = 2 * Q * K * B
@@ -88,14 +87,9 @@ def tile_fast_tucker_taylor_pa_t_kernel(tc, z, G2, grad_out, out):
             raw[q] = loads.tile([P, PACK, LOAD], BF16, name="raw")
             nc.sync.dma_start(out=raw[q][:], in_=g_rows[:, :, q * LOAD : (q + 1) * LOAD])
 
-        def regroup_on_vector(q):
+        def regroup_quad(q):
             grouped[q] = stage.tile([P, LOAD, PACK], BF16, align_bytes=64, name="grouped")
-            cut = VECTOR_REGROUPS
-            regroup(nc.vector.tensor_copy, grouped[q][:, :cut, :], raw[q][:, :, :cut])
-
-        def regroup_on_scalar(q):
-            cut = VECTOR_REGROUPS
-            regroup(nc.scalar.copy, grouped[q][:, cut:, :], raw[q][:, :, cut:])
+            regroup(nc.vector.tensor_copy, grouped[q][:], raw[q][:])
 
         def quantise(q):
             codes[q] = operand.tile([P, LOAD], U32, align_bytes=64, name="codes")
@@ -197,7 +191,7 @@ def tile_fast_tucker_taylor_pa_t_kernel(tc, z, G2, grad_out, out):
                 (u_part.rearrange("p t c b -> p t b c"), 1),
             )[i]
             prod[g, i] = products.tile([P, R, GROUP_TILES, R], F32, name="prod")
-            nc.vector.tensor_tensor(
+            nc.gpsimd.tensor_tensor(
                 out=prod[g, i][:].rearrange("p k t r -> p t k r"),
                 in0=first_sum,
                 in1=z_t[:, tiles, factor, :].unsqueeze(3).to_broadcast([P, GROUP_TILES, R, R]),
@@ -233,8 +227,7 @@ def tile_fast_tucker_taylor_pa_t_kernel(tc, z, G2, grad_out, out):
 
         g2_grouped = keep.tile([P, K, PACK], BF16, align_bytes=64)
         regroup(nc.vector.tensor_copy, g2_grouped[:], g2_raw[:])
-        regroup_on_vector(0)
-        regroup_on_scalar(0)
+        regroup_quad(0)
         nc.vector.quantize_mx(
             out=g2_codes[:].bitcast(E4M3_X4),
             scales=g2_scales[:],
@@ -250,8 +243,7 @@ def tile_fast_tucker_taylor_pa_t_kernel(tc, z, G2, grad_out, out):
                 out=z_t[:, :, i, :].rearrange("p (t g) r -> p g t r", g=R),
                 in_=z_bank[:].rearrange("p g (r t) -> p g t r", t=GROUP_TILES),
             )
-        regroup_on_vector(1)
-        regroup_on_scalar(1)
+        regroup_quad(1)
         quantise(0)
         multiply(0, 0, vector_banks)
         multiply(0, 1, vector_banks)
@@ -290,8 +282,7 @@ def tile_fast_tucker_taylor_pa_t_kernel(tc, z, G2, grad_out, out):
                 second_product(g, i)
                 second_sum(g, i)
             if quad(q + 2):
-                regroup_on_vector(q + 2)
-                regroup_on_scalar(q + 2)
+                regroup_quad(q + 2)
             if quad(q):
                 chains(q)
             if g >= 0 and i == 2:

@@ -181,20 +181,22 @@ def tile_fast_tucker_taylor_pa_t_kernel(tc, z, G2, grad_out, out):
                 in_=back[q][:],
             )
 
-        def second_product(g, i):
-            tiles = slice(g * GROUP_TILES, (g + 1) * GROUP_TILES)
-            t_part = part[g][:, 0].rearrange("p t (b a) -> p t b a", a=R)
-            u_part = part[g][:, 1].rearrange("p t (c b) -> p t c b", b=R)
+        def second_product(q, i):
+            g, k = q // GROUP_QUADS, (q % GROUP_QUADS) * QUAD
+            tiles = slice(q * QUAD, (q + 1) * QUAD)
+            t_part = part[g][:, 0, k : k + QUAD].rearrange("p t (b a) -> p t b a", a=R)
+            u_part = part[g][:, 1, k : k + QUAD].rearrange("p t (c b) -> p t c b", b=R)
             first_sum, factor = (
                 (t_part, 1),
                 (u_part, 2),
                 (u_part.rearrange("p t c b -> p t b c"), 1),
             )[i]
-            prod[g, i] = products.tile([P, R, GROUP_TILES, R], F32, name="prod")
+            if k == 0:
+                prod[g, i] = products.tile([P, R, GROUP_TILES, R], F32, name="prod%d" % i)
             nc.gpsimd.tensor_tensor(
-                out=prod[g, i][:].rearrange("p k t r -> p t k r"),
+                out=prod[g, i][:, :, k : k + QUAD, :].rearrange("p k t r -> p t k r"),
                 in0=first_sum,
-                in1=z_t[:, tiles, factor, :].unsqueeze(3).to_broadcast([P, GROUP_TILES, R, R]),
+                in1=z_t[:, tiles, factor, :].unsqueeze(3).to_broadcast([P, QUAD, R, R]),
                 op=MULT,
             )
 
@@ -252,12 +254,10 @@ def tile_fast_tucker_taylor_pa_t_kernel(tc, z, G2, grad_out, out):
         def quad(q):
             return 0 <= q < N_QUADS
 
-        for q in range(N_QUADS + GROUP_QUADS + 1):
-            g, i = divmod(q - GROUP_QUADS - 1, GROUP_QUADS)
+        for q in range(N_QUADS + 3):
+            g, phase = divmod(q - GROUP_QUADS, GROUP_QUADS)
             if quad(q + LOADS_AHEAD):
                 load(q + LOADS_AHEAD)
-            if g >= 0 and i == 3:
-                store(g)
             if quad(q + 1):
                 quantise(q + 1)
             if quad(q - 1):
@@ -267,6 +267,9 @@ def tile_fast_tucker_taylor_pa_t_kernel(tc, z, G2, grad_out, out):
             if quad(q + 1):
                 multiply(q + 1, 0, vector_banks)
                 multiply(q + 1, 1, vector_banks)
+            if g >= 0 and phase == 2:
+                copy_result(g)
+                store(g)
             if quad(q):
                 weigh(q, 0)
             if quad(q + 1):
@@ -278,12 +281,12 @@ def tile_fast_tucker_taylor_pa_t_kernel(tc, z, G2, grad_out, out):
                 weigh(q, 1)
             if quad(q - 1):
                 copy_back(q - 1)
-            if g >= 0 and i < 3:
-                second_product(g, i)
-                second_sum(g, i)
+                for i in range(3):
+                    second_product(q - 1, i)
+            if g >= 0 and phase == 1:
+                for i in range(3):
+                    second_sum(g, i)
             if quad(q + 2):
                 regroup_quad(q + 2)
             if quad(q):
                 chains(q)
-            if g >= 0 and i == 2:
-                copy_result(g)

@@ -48,13 +48,10 @@ def slice_a(d_bank, a):
     return d_bank[:].rearrange("p (cb a) -> p cb a", a=R)[:, :, a]
 
 
-def accumulate(nc, acc, d_slice, weight, first):
-    if first:
-        nc.vector.tensor_scalar_mul(out=acc, in0=d_slice, scalar1=weight)
-    else:
-        nc.vector.scalar_tensor_tensor(
-            out=acc, in0=d_slice, scalar=weight, in1=acc, op0=MULT, op1=ADD
-        )
+def accumulate(nc, acc, d_slice, weight, so_far):
+    nc.vector.scalar_tensor_tensor(
+        out=acc, in0=d_slice, scalar=weight, in1=so_far, op0=MULT, op1=ADD
+    )
 
 
 def tile_fast_tucker_taylor_pa_t_kernel(tc, z, G2, grad_out, out):
@@ -81,7 +78,7 @@ def tile_fast_tucker_taylor_pa_t_kernel(tc, z, G2, grad_out, out):
 
         raw, grouped, codes, scales = {}, {}, {}, {}
         d_banks, terms, turned, turned_sb, back = {}, {}, {}, {}, {}
-        part, prod, sums, result = {}, {}, {}, {}
+        part, prod, sums, result, seeds = {}, {}, {}, {}, {}
 
         def load(q):
             raw[q] = loads.tile([P, PACK, LOAD], BF16, name="raw")
@@ -121,16 +118,25 @@ def tile_fast_tucker_taylor_pa_t_kernel(tc, z, G2, grad_out, out):
 
         def chains(q):
             group_part, k = part_of(q)
-            for step in range(R):
+            for step in range(R - 1):
                 for s in range(2):
                     tile_no = q * QUAD + s
-                    accumulate(
-                        nc, group_part[:, 0, k + s, :], slice_c(d_banks[q, s], step),
-                        z_t[:, tile_no, 2, step : step + 1], step == 0,
-                    )
-                    accumulate(
-                        nc, group_part[:, 1, k + s, :], slice_a(d_banks[q, s], step),
-                        z_t[:, tile_no, 0, step : step + 1], step == 0,
+                    for which, take, factor in ((0, slice_c, 2), (1, slice_a, 0)):
+                        acc = group_part[:, which, k + s, :]
+                        accumulate(
+                            nc, acc, take(d_banks[q, s], step),
+                            z_t[:, tile_no, factor, step : step + 1],
+                            seeds[q][:, which, s, :] if step == 0 else acc,
+                        )
+
+        def seed(q):
+            seeds[q] = weighted.tile([P, 2, 2, RR], F32, name="seeds")
+            for s in range(2):
+                tile_no = q * QUAD + s
+                for which, take, factor in ((0, slice_c, 2), (1, slice_a, 0)):
+                    nc.scalar.activation(
+                        out=seeds[q][:, which, s, :], in_=take(d_banks[q, s], R - 1), func=COPY,
+                        scale=z_t[:, tile_no, factor, R - 1 : R],
                     )
 
         def weigh(q, s):
@@ -250,6 +256,7 @@ def tile_fast_tucker_taylor_pa_t_kernel(tc, z, G2, grad_out, out):
         multiply(0, 0, vector_banks)
         multiply(0, 1, vector_banks)
         multiply(0, 2, scalar_banks)
+        seed(0)
 
         def quad(q):
             return 0 <= q < N_QUADS
@@ -283,6 +290,8 @@ def tile_fast_tucker_taylor_pa_t_kernel(tc, z, G2, grad_out, out):
                 copy_back(q - 1)
                 for i in range(3):
                     second_product(q - 1, i)
+            if quad(q + 1):
+                seed(q + 1)
             if g >= 0 and phase == 1:
                 for i in range(3):
                     second_sum(g, i)

@@ -67,7 +67,7 @@ def tile_fast_tucker_taylor_pa_t_kernel(tc, z, G2, grad_out, out):
         vector_banks = ctx.enter_context(tc.psum_pool(name="vector_banks", bufs=4))
         scalar_banks = ctx.enter_context(tc.psum_pool(name="scalar_banks", bufs=2))
         turn_bank = ctx.enter_context(tc.psum_pool(name="turn_bank", bufs=1))
-        sums_bank = ctx.enter_context(tc.psum_pool(name="sums_bank", bufs=1))
+        back_bank = ctx.enter_context(tc.psum_pool(name="back_bank", bufs=1))
         ctx.enter_context(tc.manual_schedule())
 
         g_rows = grad_out.rearrange("(p j) n -> p j n", j=PACK)
@@ -78,7 +78,7 @@ def tile_fast_tucker_taylor_pa_t_kernel(tc, z, G2, grad_out, out):
 
         raw, grouped, codes, scales = {}, {}, {}, {}
         d_banks, terms, turned, turned_sb, back = {}, {}, {}, {}, {}
-        part, prod, sums, result, seeds = {}, {}, {}, {}, {}
+        part, halved, sums, result, seeds = {}, {}, {}, {}, {}
 
         def load(q):
             raw[q] = loads.tile([P, PACK, LOAD], BF16, name="raw")
@@ -176,7 +176,7 @@ def tile_fast_tucker_taylor_pa_t_kernel(tc, z, G2, grad_out, out):
             nc.scalar.copy(out=turned_sb[q][:], in_=turned[q][:])
 
         def turn_back(q):
-            back[q] = turn_bank.tile([P, 2, TILE], F32, tag="turn", name="back")
+            back[q] = back_bank.tile([P, 2, TILE], F32, tag="back", name="back")
             for which in range(2):
                 nc.tensor.transpose(back[q][:, which, :], turned_sb[q][:, which, :], ident[:])
 
@@ -187,29 +187,40 @@ def tile_fast_tucker_taylor_pa_t_kernel(tc, z, G2, grad_out, out):
                 in_=back[q][:],
             )
 
-        def second_product(q, i):
+        def second_level(q):
             g, k = q // GROUP_QUADS, (q % GROUP_QUADS) * QUAD
             tiles = slice(q * QUAD, (q + 1) * QUAD)
             t_part = part[g][:, 0, k : k + QUAD].rearrange("p t (b a) -> p t b a", a=R)
             u_part = part[g][:, 1, k : k + QUAD].rearrange("p t (c b) -> p t c b", b=R)
-            first_sum, factor = (
-                (t_part, 1),
-                (u_part, 2),
-                (u_part.rearrange("p t c b -> p t b c"), 1),
-            )[i]
+            prod = products.tile([P, 3, R, QUAD, R], F32, name="prod")
+            for i, first_sum, factor in (
+                (0, t_part, 1),
+                (1, u_part, 2),
+                (2, u_part.rearrange("p t c b -> p t b c"), 1),
+            ):
+                nc.gpsimd.tensor_tensor(
+                    out=prod[:, i].rearrange("p k t r -> p t k r"),
+                    in0=first_sum,
+                    in1=z_t[:, tiles, factor, :].unsqueeze(3).to_broadcast([P, QUAD, R, R]),
+                    op=MULT,
+                )
             if k == 0:
-                prod[g, i] = products.tile([P, R, GROUP_TILES, R], F32, name="prod%d" % i)
+                halved[g] = products.tile([P, 3, R // 2, GROUP_TILES, R], F32, name="halved")
             nc.gpsimd.tensor_tensor(
-                out=prod[g, i][:, :, k : k + QUAD, :].rearrange("p k t r -> p t k r"),
-                in0=first_sum,
-                in1=z_t[:, tiles, factor, :].unsqueeze(3).to_broadcast([P, QUAD, R, R]),
-                op=MULT,
+                out=halved[g][:, :, :, k : k + QUAD, :].rearrange("p i k t r -> p i k (t r)"),
+                in0=prod[:, :, : R // 2].rearrange("p i k t r -> p i k (t r)"),
+                in1=prod[:, :, R // 2 :].rearrange("p i k t r -> p i k (t r)"),
+                op=ADD,
             )
 
-        def second_sum(g, i):
-            if i == 0:
-                sums[g] = sums_bank.tile([P, 3, TILE], F32, name="sums")
-            add_up(sums[g][:, i, :], prod[g, i])
+        def second_sum(g):
+            sums[g] = back_bank.tile([P, 3, TILE], F32, tag="back", name="sums")
+            for i in range(3):
+                for k in range(R // 2):
+                    nc.tensor.matmul(
+                        out=sums[g][:, i, :], lhsT=halved[g][:, i, k].rearrange("p t r -> p (t r)"),
+                        rhs=ident[:], is_transpose=True, start=(k == 0), stop=(k == R // 2 - 1),
+                    )
 
         def copy_result(g):
             result[g] = products.tile([P, 3, TILE], F32, name="result")
@@ -262,39 +273,36 @@ def tile_fast_tucker_taylor_pa_t_kernel(tc, z, G2, grad_out, out):
             return 0 <= q < N_QUADS
 
         for q in range(N_QUADS + 3):
-            g, phase = divmod(q - GROUP_QUADS, GROUP_QUADS)
+            g, phase = divmod(q - GROUP_QUADS - 2, GROUP_QUADS)
             if quad(q + LOADS_AHEAD):
                 load(q + LOADS_AHEAD)
             if quad(q + 1):
                 quantise(q + 1)
-            if quad(q - 1):
-                add_terms(q - 1)
             if quad(q):
                 multiply(q, 3, scalar_banks)
-            if quad(q + 1):
-                multiply(q + 1, 0, vector_banks)
-                multiply(q + 1, 1, vector_banks)
-            if g >= 0 and phase == 2:
-                copy_result(g)
-                store(g)
+            if quad(q - 2):
+                turn_back(q - 2)
+            if quad(q - 1):
+                add_terms(q - 1)
             if quad(q):
                 weigh(q, 0)
             if quad(q + 1):
                 multiply(q + 1, 2, scalar_banks)
-            if quad(q - 1):
-                copy_turned(q - 1)
-                turn_back(q - 1)
+                multiply(q + 1, 0, vector_banks)
+                multiply(q + 1, 1, vector_banks)
+            if quad(q - 2):
+                copy_back(q - 2)
+                second_level(q - 2)
             if quad(q):
                 weigh(q, 1)
             if quad(q - 1):
-                copy_back(q - 1)
-                for i in range(3):
-                    second_product(q - 1, i)
+                copy_turned(q - 1)
             if quad(q + 1):
                 seed(q + 1)
-            if g >= 0 and phase == 1:
-                for i in range(3):
-                    second_sum(g, i)
+            if g >= 0 and phase == 0:
+                second_sum(g)
+                copy_result(g)
+                store(g)
             if quad(q + 2):
                 regroup_quad(q + 2)
             if quad(q):

@@ -78,7 +78,7 @@ def tile_fast_tucker_taylor_pa_t_kernel(tc, z, G2, grad_out, out):
 
         raw, grouped, codes, scales = {}, {}, {}, {}
         d_banks, terms, turned, turned_sb, back = {}, {}, {}, {}, {}
-        part, halved, sums, result, seeds = {}, {}, {}, {}, {}
+        part, halved, sums, result = {}, {}, {}, {}
 
         def load(q):
             raw[q] = loads.tile([P, PACK, LOAD], BF16, name="raw")
@@ -118,26 +118,16 @@ def tile_fast_tucker_taylor_pa_t_kernel(tc, z, G2, grad_out, out):
 
         def chains(q):
             group_part, k = part_of(q)
-            for step in range(R - 1):
+            for step in range(R):
                 for s in range(2):
                     tile_no = q * QUAD + s
                     for which, take, factor in ((0, slice_c, 2), (1, slice_a, 0)):
                         acc = group_part[:, which, k + s, :]
-                        accumulate(
-                            nc, acc, take(d_banks[q, s], step),
-                            z_t[:, tile_no, factor, step : step + 1],
-                            seeds[q][:, which, s, :] if step == 0 else acc,
-                        )
-
-        def seed(q):
-            seeds[q] = weighted.tile([P, 2, 2, RR], F32, name="seeds")
-            for s in range(2):
-                tile_no = q * QUAD + s
-                for which, take, factor in ((0, slice_c, 2), (1, slice_a, 0)):
-                    nc.scalar.activation(
-                        out=seeds[q][:, which, s, :], in_=take(d_banks[q, s], R - 1), func=COPY,
-                        scale=z_t[:, tile_no, factor, R - 1 : R],
-                    )
+                        weight = z_t[:, tile_no, factor, step : step + 1]
+                        if step == 0:
+                            nc.vector.tensor_scalar_mul(out=acc, in0=take(d_banks[q, s], step), scalar1=weight)
+                        else:
+                            accumulate(nc, acc, take(d_banks[q, s], step), weight, acc)
 
         def weigh(q, s):
             if s == 0:
@@ -267,7 +257,6 @@ def tile_fast_tucker_taylor_pa_t_kernel(tc, z, G2, grad_out, out):
         multiply(0, 0, vector_banks)
         multiply(0, 1, vector_banks)
         multiply(0, 2, scalar_banks)
-        seed(0)
 
         def quad(q):
             return 0 <= q < N_QUADS
@@ -286,21 +275,20 @@ def tile_fast_tucker_taylor_pa_t_kernel(tc, z, G2, grad_out, out):
                 add_terms(q - 1)
             if quad(q):
                 weigh(q, 0)
+            if quad(q - 2):
+                copy_back(q - 2)
+                second_level(q - 2)
+            if g >= 0 and phase == 0:
+                second_sum(g)
             if quad(q + 1):
                 multiply(q + 1, 2, scalar_banks)
                 multiply(q + 1, 0, vector_banks)
                 multiply(q + 1, 1, vector_banks)
-            if quad(q - 2):
-                copy_back(q - 2)
-                second_level(q - 2)
             if quad(q):
                 weigh(q, 1)
             if quad(q - 1):
                 copy_turned(q - 1)
-            if quad(q + 1):
-                seed(q + 1)
             if g >= 0 and phase == 0:
-                second_sum(g)
                 copy_result(g)
                 store(g)
             if quad(q + 2):

@@ -28,7 +28,11 @@ QUAD = 4
 LOAD = QUAD * TILE
 N_QUADS = B // LOAD
 GROUP_QUADS = GROUP_TILES // QUAD
-LOADS_AHEAD = 4
+LAST_GROUP = N_QUADS // GROUP_QUADS - 1
+BLOCK_QUADS = 4
+BLOCK = BLOCK_QUADS * LOAD
+N_BLOCKS = B // BLOCK
+BLOCKS_IN_FLIGHT = 3
 
 FLOPS = 2 * Q * K * B
 
@@ -58,7 +62,7 @@ def tile_fast_tucker_taylor_pa_t_kernel(tc, z, G2, grad_out, out):
     nc = tc.nc
     with ExitStack() as ctx:
         keep = ctx.enter_context(tc.tile_pool(name="keep", bufs=1))
-        loads = ctx.enter_context(tc.tile_pool(name="loads", bufs=LOADS_AHEAD))
+        loads = ctx.enter_context(tc.tile_pool(name="loads", bufs=BLOCKS_IN_FLIGHT))
         stage = ctx.enter_context(tc.tile_pool(name="stage", bufs=2))
         operand = ctx.enter_context(tc.tile_pool(name="operand", bufs=3))
         partial = ctx.enter_context(tc.tile_pool(name="partial", bufs=2))
@@ -78,15 +82,19 @@ def tile_fast_tucker_taylor_pa_t_kernel(tc, z, G2, grad_out, out):
 
         raw, grouped, codes, scales = {}, {}, {}, {}
         d_banks, terms, turned, turned_sb, back = {}, {}, {}, {}, {}
-        part, halved, sums, result = {}, {}, {}, {}
+        part, prod, sums, result = {}, {}, {}, {}
 
-        def load(q):
-            raw[q] = loads.tile([P, PACK, LOAD], BF16, name="raw")
-            nc.sync.dma_start(out=raw[q][:], in_=g_rows[:, :, q * LOAD : (q + 1) * LOAD])
+        def load(block):
+            raw[block] = loads.tile([P, PACK, BLOCK], BF16, name="raw")
+            nc.sync.dma_start(out=raw[block][:], in_=g_rows[:, :, block * BLOCK : (block + 1) * BLOCK])
 
         def regroup_quad(q):
             grouped[q] = stage.tile([P, LOAD, PACK], BF16, align_bytes=64, name="grouped")
-            regroup(nc.vector.tensor_copy, grouped[q][:], raw[q][:])
+            block, place = divmod(q, BLOCK_QUADS)
+            regroup(
+                nc.vector.tensor_copy, grouped[q][:],
+                raw[block][:, :, place * LOAD : (place + 1) * LOAD],
+            )
 
         def quantise(q):
             codes[q] = operand.tile([P, LOAD], U32, align_bytes=64, name="codes")
@@ -177,44 +185,37 @@ def tile_fast_tucker_taylor_pa_t_kernel(tc, z, G2, grad_out, out):
                 in_=back[q][:],
             )
 
-        def second_level(q):
+        def second_products(q):
             g, k = q // GROUP_QUADS, (q % GROUP_QUADS) * QUAD
             tiles = slice(q * QUAD, (q + 1) * QUAD)
             t_part = part[g][:, 0, k : k + QUAD].rearrange("p t (b a) -> p t b a", a=R)
             u_part = part[g][:, 1, k : k + QUAD].rearrange("p t (c b) -> p t c b", b=R)
-            prod = products.tile([P, 3, R, QUAD, R], F32, name="prod")
             for i, first_sum, factor in (
                 (0, t_part, 1),
                 (1, u_part, 2),
                 (2, u_part.rearrange("p t c b -> p t b c"), 1),
             ):
-                nc.gpsimd.tensor_tensor(
-                    out=prod[:, i].rearrange("p k t r -> p t k r"),
+                if k == 0:
+                    prod[g, i] = products.tile([P, R, GROUP_TILES, R], F32, name="prod%d" % i)
+                engine = nc.vector if q == N_QUADS - 1 else nc.gpsimd
+                engine.tensor_tensor(
+                    out=prod[g, i][:, :, k : k + QUAD, :].rearrange("p k t r -> p t k r"),
                     in0=first_sum,
                     in1=z_t[:, tiles, factor, :].unsqueeze(3).to_broadcast([P, QUAD, R, R]),
                     op=MULT,
                 )
-            if k == 0:
-                halved[g] = products.tile([P, 3, R // 2, GROUP_TILES, R], F32, name="halved")
-            nc.gpsimd.tensor_tensor(
-                out=halved[g][:, :, :, k : k + QUAD, :].rearrange("p i k t r -> p i k (t r)"),
-                in0=prod[:, :, : R // 2].rearrange("p i k t r -> p i k (t r)"),
-                in1=prod[:, :, R // 2 :].rearrange("p i k t r -> p i k (t r)"),
-                op=ADD,
-            )
 
-        def second_sum(g):
-            sums[g] = back_bank.tile([P, 3, TILE], F32, tag="back", name="sums")
-            for i in range(3):
-                for k in range(R // 2):
-                    nc.tensor.matmul(
-                        out=sums[g][:, i, :], lhsT=halved[g][:, i, k].rearrange("p t r -> p (t r)"),
-                        rhs=ident[:], is_transpose=True, start=(k == 0), stop=(k == R // 2 - 1),
-                    )
+        def second_sum(g, i):
+            if g == LAST_GROUP:
+                sums[g, i] = vector_banks.tile([P, TILE], F32, tag="bank", name="last_sums")
+            else:
+                sums[g, i] = back_bank.tile([P, TILE], F32, tag="back", name="sums")
+            add_up(sums[g, i][:], prod[g, i])
 
-        def copy_result(g):
-            result[g] = products.tile([P, 3, TILE], F32, name="result")
-            nc.scalar.copy(out=result[g][:], in_=sums[g][:])
+        def copy_result(g, i):
+            if i == 0:
+                result[g] = products.tile([P, 3, TILE], F32, name="result")
+            nc.scalar.copy(out=result[g][:, i, :], in_=sums[g, i][:])
 
         def store(g):
             for r in range(R):
@@ -225,11 +226,16 @@ def tile_fast_tucker_taylor_pa_t_kernel(tc, z, G2, grad_out, out):
 
         g2_raw = keep.tile([P, PACK, K], BF16)
         nc.sync.dma_start(out=g2_raw[:], in_=G2.rearrange("(p j) k -> p j k", j=PACK))
-        load(0)
+        raw[0] = loads.tile([P, PACK, BLOCK], BF16, name="raw")
+        first_cols = slice(0, LOAD)
+        nc.sync.dma_start(out=raw[0][:, :, first_cols], in_=g_rows[:, :, first_cols])
         z_rows = keep.tile([P, 3, B // GROUP_TILES], BF16)
         nc.sync.dma_start(out=z_rows[:], in_=z.rearrange("i r (t x) -> (r t) i x", t=GROUP_TILES))
-        for q in range(1, LOADS_AHEAD):
-            load(q)
+        for place in range(1, BLOCK_QUADS):
+            cols = slice(place * LOAD, (place + 1) * LOAD)
+            nc.sync.dma_start(out=raw[0][:, :, cols], in_=g_rows[:, :, cols])
+        for block in range(1, BLOCKS_IN_FLIGHT):
+            load(block)
         ident_bf = keep.tile([P, P], BF16)
         make_identity(nc, ident_bf[:])
         make_identity(nc, ident[:])
@@ -261,10 +267,11 @@ def tile_fast_tucker_taylor_pa_t_kernel(tc, z, G2, grad_out, out):
         def quad(q):
             return 0 <= q < N_QUADS
 
-        for q in range(N_QUADS + 3):
-            g, phase = divmod(q - GROUP_QUADS - 2, GROUP_QUADS)
-            if quad(q + LOADS_AHEAD):
-                load(q + LOADS_AHEAD)
+        for q in range(N_QUADS + 2):
+            g, i = divmod(q - GROUP_QUADS - 2, GROUP_QUADS)
+            summing = 0 <= g < LAST_GROUP and i < 3
+            if q % BLOCK_QUADS == 2 and q // BLOCK_QUADS + BLOCKS_IN_FLIGHT < N_BLOCKS:
+                load(q // BLOCK_QUADS + BLOCKS_IN_FLIGHT)
             if quad(q + 1):
                 quantise(q + 1)
             if quad(q):
@@ -277,9 +284,9 @@ def tile_fast_tucker_taylor_pa_t_kernel(tc, z, G2, grad_out, out):
                 weigh(q, 0)
             if quad(q - 2):
                 copy_back(q - 2)
-                second_level(q - 2)
-            if g >= 0 and phase == 0:
-                second_sum(g)
+                second_products(q - 2)
+            if summing:
+                second_sum(g, i)
             if quad(q + 1):
                 multiply(q + 1, 2, scalar_banks)
                 multiply(q + 1, 0, vector_banks)
@@ -288,10 +295,16 @@ def tile_fast_tucker_taylor_pa_t_kernel(tc, z, G2, grad_out, out):
                 weigh(q, 1)
             if quad(q - 1):
                 copy_turned(q - 1)
-            if g >= 0 and phase == 0:
-                copy_result(g)
-                store(g)
+            if summing:
+                copy_result(g, i)
+                if i == 2:
+                    store(g)
             if quad(q + 2):
                 regroup_quad(q + 2)
             if quad(q):
                 chains(q)
+        for i in range(3):
+            second_sum(LAST_GROUP, i)
+        for i in range(3):
+            copy_result(LAST_GROUP, i)
+        store(LAST_GROUP)

@@ -80,7 +80,7 @@ def tile_fast_tucker_taylor_pa_t_kernel(tc, z, G2, grad_out, out):
         z_t = keep.tile([P, N_TILES, 3, R], F32)
         ident = keep.tile([P, P], F32)
 
-        raw, grouped, codes, scales = {}, {}, {}, {}
+        raw, first_raw, grouped, codes, scales = {}, {}, {}, {}, {}
         d_banks, terms, turned, turned_sb, back = {}, {}, {}, {}, {}
         part, prod, sums, result = {}, {}, {}, {}
 
@@ -88,13 +88,18 @@ def tile_fast_tucker_taylor_pa_t_kernel(tc, z, G2, grad_out, out):
             raw[block] = loads.tile([P, PACK, BLOCK], BF16, name="raw")
             nc.sync.dma_start(out=raw[block][:], in_=g_rows[:, :, block * BLOCK : (block + 1) * BLOCK])
 
+        def load_first(q):
+            first_raw[q] = keep.tile([P, PACK, LOAD], BF16, name="first_raw%d" % q)
+            nc.sync.dma_start(out=first_raw[q][:], in_=g_rows[:, :, q * LOAD : (q + 1) * LOAD])
+
         def regroup_quad(q):
             grouped[q] = stage.tile([P, LOAD, PACK], BF16, align_bytes=64, name="grouped")
             block, place = divmod(q, BLOCK_QUADS)
-            regroup(
-                nc.vector.tensor_copy, grouped[q][:],
-                raw[block][:, :, place * LOAD : (place + 1) * LOAD],
-            )
+            if block == 0:
+                source = first_raw[q][:]
+            else:
+                source = raw[block][:, :, place * LOAD : (place + 1) * LOAD]
+            regroup(nc.vector.tensor_copy, grouped[q][:], source)
 
         def quantise(q):
             codes[q] = operand.tile([P, LOAD], U32, align_bytes=64, name="codes")
@@ -226,15 +231,12 @@ def tile_fast_tucker_taylor_pa_t_kernel(tc, z, G2, grad_out, out):
 
         g2_raw = keep.tile([P, PACK, K], BF16)
         nc.sync.dma_start(out=g2_raw[:], in_=G2.rearrange("(p j) k -> p j k", j=PACK))
-        raw[0] = loads.tile([P, PACK, BLOCK], BF16, name="raw")
-        first_cols = slice(0, LOAD)
-        nc.sync.dma_start(out=raw[0][:, :, first_cols], in_=g_rows[:, :, first_cols])
+        load_first(0)
         z_rows = keep.tile([P, 3, B // GROUP_TILES], BF16)
         nc.sync.dma_start(out=z_rows[:], in_=z.rearrange("i r (t x) -> (r t) i x", t=GROUP_TILES))
-        for place in range(1, BLOCK_QUADS):
-            cols = slice(place * LOAD, (place + 1) * LOAD)
-            nc.sync.dma_start(out=raw[0][:, :, cols], in_=g_rows[:, :, cols])
-        for block in range(1, BLOCKS_IN_FLIGHT):
+        for q in range(1, BLOCK_QUADS):
+            load_first(q)
+        for block in range(1, 1 + BLOCKS_IN_FLIGHT):
             load(block)
         ident_bf = keep.tile([P, P], BF16)
         make_identity(nc, ident_bf[:])
@@ -270,7 +272,7 @@ def tile_fast_tucker_taylor_pa_t_kernel(tc, z, G2, grad_out, out):
         for q in range(N_QUADS + 2):
             g, i = divmod(q - GROUP_QUADS - 2, GROUP_QUADS)
             summing = 0 <= g < LAST_GROUP and i < 3
-            if q % BLOCK_QUADS == 2 and q // BLOCK_QUADS + BLOCKS_IN_FLIGHT < N_BLOCKS:
+            if q % BLOCK_QUADS == 2 and 1 <= q // BLOCK_QUADS < N_BLOCKS - BLOCKS_IN_FLIGHT:
                 load(q // BLOCK_QUADS + BLOCKS_IN_FLIGHT)
             if quad(q + 1):
                 quantise(q + 1)

@@ -33,6 +33,7 @@ BLOCK_QUADS = 4
 BLOCK = BLOCK_QUADS * LOAD
 N_BLOCKS = B // BLOCK
 BLOCKS_IN_FLIGHT = 3
+DOUBLED = 2
 
 FLOPS = 2 * Q * K * B
 
@@ -64,9 +65,9 @@ def tile_fast_tucker_taylor_pa_t_kernel(tc, z, G2, grad_out, out):
         keep = ctx.enter_context(tc.tile_pool(name="keep", bufs=1))
         loads = ctx.enter_context(tc.tile_pool(name="loads", bufs=BLOCKS_IN_FLIGHT))
         stage = ctx.enter_context(tc.tile_pool(name="stage", bufs=2))
-        operand = ctx.enter_context(tc.tile_pool(name="operand", bufs=3))
+        operand = ctx.enter_context(tc.tile_pool(name="operand", bufs=4))
         partial = ctx.enter_context(tc.tile_pool(name="partial", bufs=2))
-        weighted = ctx.enter_context(tc.tile_pool(name="weighted", bufs=2))
+        weighted = ctx.enter_context(tc.tile_pool(name="weighted", bufs=3))
         products = ctx.enter_context(tc.tile_pool(name="products", bufs=2))
         vector_banks = ctx.enter_context(tc.psum_pool(name="vector_banks", bufs=4))
         scalar_banks = ctx.enter_context(tc.psum_pool(name="scalar_banks", bufs=2))
@@ -110,18 +111,19 @@ def tile_fast_tucker_taylor_pa_t_kernel(tc, z, G2, grad_out, out):
                 in_=grouped[q][:].rearrange("p w j -> p (w j)"),
             )
 
-        def multiply(q, s, pool):
+        def multiply(q, s, pool, times=1):
             cols = slice(s * TILE, (s + 1) * TILE)
             d_banks[q, s] = pool.tile([P, K], F32, tag="bank", name="d_bank")
-            nc.tensor.matmul_mx(
-                out=d_banks[q, s][:],
-                lhsT=codes[q][:, cols].bitcast(E5M2_X4),
-                lhsT_scale=scales[q][:, cols],
-                rhs=g2_codes[:].bitcast(E4M3_X4),
-                rhs_scale=g2_scales[:],
-                start=True,
-                stop=True,
-            )
+            for again in range(times):
+                nc.tensor.matmul_mx(
+                    out=d_banks[q, s][:],
+                    lhsT=codes[q][:, cols].bitcast(E5M2_X4),
+                    lhsT_scale=scales[q][:, cols],
+                    rhs=g2_codes[:].bitcast(E4M3_X4),
+                    rhs_scale=g2_scales[:],
+                    start=True,
+                    stop=True,
+                )
 
         def part_of(q):
             g = q // GROUP_QUADS
@@ -142,24 +144,18 @@ def tile_fast_tucker_taylor_pa_t_kernel(tc, z, G2, grad_out, out):
                         else:
                             accumulate(nc, acc, take(d_banks[q, s], step), weight, acc)
 
-        def weigh(q, s):
-            if s == 0:
+        def weigh(q, s, which):
+            if (s, which) == (0, 0):
                 terms[q] = (
                     weighted.tile([P, R, 2, RR], F32, name="t_terms"),
                     weighted.tile([P, R, 2, RR], F32, name="u_terms"),
                 )
-            t_terms, u_terms = terms[q]
             tile_no = q * QUAD + 2 + s
-            d_bank = d_banks[q, 2 + s]
+            take, factor = ((slice_c, 2), (slice_a, 0))[which]
             for step in range(R):
                 nc.scalar.activation(
-                    out=t_terms[:, step, s, :], in_=slice_c(d_bank, step), func=COPY,
-                    scale=z_t[:, tile_no, 2, step : step + 1],
-                )
-            for step in range(R):
-                nc.scalar.activation(
-                    out=u_terms[:, step, s, :], in_=slice_a(d_bank, step), func=COPY,
-                    scale=z_t[:, tile_no, 0, step : step + 1],
+                    out=terms[q][which][:, step, s, :], in_=take(d_banks[q, 2 + s], step), func=COPY,
+                    scale=z_t[:, tile_no, factor, step : step + 1],
                 )
 
         def add_up(bank_cols, slabs):
@@ -169,10 +165,10 @@ def tile_fast_tucker_taylor_pa_t_kernel(tc, z, G2, grad_out, out):
                     is_transpose=True, start=(step == 0), stop=(step == R - 1),
                 )
 
-        def add_terms(q):
-            turned[q] = turn_bank.tile([P, 2, TILE], F32, tag="turn", name="turned")
-            for which in range(2):
-                add_up(turned[q][:, which, :], terms[q][which])
+        def add_terms(q, which):
+            if which == 0:
+                turned[q] = turn_bank.tile([P, 2, TILE], F32, tag="turn", name="turned")
+            add_up(turned[q][:, which, :], terms[q][which])
 
         def copy_turned(q):
             turned_sb[q] = weighted.tile([P, 2, TILE], F32, name="turned_sb")
@@ -260,49 +256,57 @@ def tile_fast_tucker_taylor_pa_t_kernel(tc, z, G2, grad_out, out):
                 out=z_t[:, :, i, :].rearrange("p (t g) r -> p g t r", g=R),
                 in_=z_bank[:].rearrange("p g (r t) -> p g t r", t=GROUP_TILES),
             )
-        regroup_quad(1)
         quantise(0)
+        regroup_quad(1)
         multiply(0, 0, vector_banks)
         multiply(0, 1, vector_banks)
         multiply(0, 2, scalar_banks)
+        regroup_quad(2)
+        quantise(1)
 
         def quad(q):
             return 0 <= q < N_QUADS
 
         for q in range(N_QUADS + 2):
-            g, i = divmod(q - GROUP_QUADS - 2, GROUP_QUADS)
+            g, i = divmod(q - GROUP_QUADS - 3, GROUP_QUADS)
             summing = 0 <= g < LAST_GROUP and i < 3
-            if q % BLOCK_QUADS == 2 and 1 <= q // BLOCK_QUADS < N_BLOCKS - BLOCKS_IN_FLIGHT:
+            if q % BLOCK_QUADS == 1 and 1 <= q // BLOCK_QUADS < N_BLOCKS - BLOCKS_IN_FLIGHT:
                 load(q // BLOCK_QUADS + BLOCKS_IN_FLIGHT)
+            if quad(q + 2):
+                quantise(q + 2)
+            if quad(q):
+                multiply(q, 3, scalar_banks, DOUBLED)
             if quad(q + 1):
-                quantise(q + 1)
+                multiply(q + 1, 0, vector_banks)
             if quad(q):
-                multiply(q, 3, scalar_banks)
+                weigh(q, 0, 0)
+                weigh(q, 0, 1)
             if quad(q - 2):
-                turn_back(q - 2)
-            if quad(q - 1):
-                add_terms(q - 1)
-            if quad(q):
-                weigh(q, 0)
-            if quad(q - 2):
-                copy_back(q - 2)
-                second_products(q - 2)
+                add_terms(q - 2, 1)
             if summing:
                 second_sum(g, i)
             if quad(q + 1):
-                multiply(q + 1, 2, scalar_banks)
-                multiply(q + 1, 0, vector_banks)
+                multiply(q + 1, 2, scalar_banks, DOUBLED)
                 multiply(q + 1, 1, vector_banks)
             if quad(q):
-                weigh(q, 1)
-            if quad(q - 1):
-                copy_turned(q - 1)
+                weigh(q, 1, 0)
+            if quad(q - 2):
+                copy_turned(q - 2)
             if summing:
                 copy_result(g, i)
                 if i == 2:
                     store(g)
-            if quad(q + 2):
-                regroup_quad(q + 2)
+            if quad(q):
+                weigh(q, 1, 1)
+            if quad(q - 2):
+                turn_back(q - 2)
+            if quad(q - 1):
+                add_terms(q - 1, 0)
+            if quad(q - 2):
+                copy_back(q - 2)
+                second_products(q - 2)
+            if quad(q + 3):
+                regroup_quad(q + 3)
             if quad(q):
                 chains(q)
         for i in range(3):

@@ -65,8 +65,8 @@ def tile_fast_tucker_taylor_pa_t_kernel(tc, z, G2, grad_out, out):
         keep = ctx.enter_context(tc.tile_pool(name="keep", bufs=1))
         loads = ctx.enter_context(tc.tile_pool(name="loads", bufs=BLOCKS_IN_FLIGHT))
         stage = ctx.enter_context(tc.tile_pool(name="stage", bufs=2))
-        operand = ctx.enter_context(tc.tile_pool(name="operand", bufs=4))
-        partial = ctx.enter_context(tc.tile_pool(name="partial", bufs=2))
+        operand = ctx.enter_context(tc.tile_pool(name="operand", bufs=5))
+        partial = ctx.enter_context(tc.tile_pool(name="partial", bufs=3))
         weighted = ctx.enter_context(tc.tile_pool(name="weighted", bufs=3))
         products = ctx.enter_context(tc.tile_pool(name="products", bufs=2))
         vector_banks = ctx.enter_context(tc.psum_pool(name="vector_banks", bufs=4))
@@ -133,16 +133,24 @@ def tile_fast_tucker_taylor_pa_t_kernel(tc, z, G2, grad_out, out):
 
         def chains(q):
             group_part, k = part_of(q)
-            for step in range(R):
+            for step in range(R - 1):
                 for s in range(2):
                     tile_no = q * QUAD + s
                     for which, take, factor in ((0, slice_c, 2), (1, slice_a, 0)):
                         acc = group_part[:, which, k + s, :]
                         weight = z_t[:, tile_no, factor, step : step + 1]
-                        if step == 0:
-                            nc.vector.tensor_scalar_mul(out=acc, in0=take(d_banks[q, s], step), scalar1=weight)
-                        else:
-                            accumulate(nc, acc, take(d_banks[q, s], step), weight, acc)
+                        accumulate(nc, acc, take(d_banks[q, s], step), weight, acc)
+
+        def seed(q):
+            group_part, k = part_of(q)
+            last = R - 1
+            for s in range(2):
+                tile_no = q * QUAD + s
+                for which, take, factor in ((0, slice_c, 2), (1, slice_a, 0)):
+                    nc.scalar.activation(
+                        out=group_part[:, which, k + s, :], in_=take(d_banks[q, s], last), func=COPY,
+                        scale=z_t[:, tile_no, factor, last : last + 1],
+                    )
 
         def weigh(q, s, which):
             if (s, which) == (0, 0):
@@ -167,12 +175,15 @@ def tile_fast_tucker_taylor_pa_t_kernel(tc, z, G2, grad_out, out):
 
         def add_terms(q, which):
             if which == 0:
-                turned[q] = turn_bank.tile([P, 2, TILE], F32, tag="turn", name="turned")
+                turned[q] = turn_bank.tile([P, 3, TILE], F32, tag="turn", name="turned")
             add_up(turned[q][:, which, :], terms[q][which])
 
         def copy_turned(q):
-            turned_sb[q] = weighted.tile([P, 2, TILE], F32, name="turned_sb")
-            nc.scalar.copy(out=turned_sb[q][:], in_=turned[q][:])
+            turned_sb[q] = weighted.tile([P, 3, TILE], F32, name="turned_sb")
+            n = 3 if q in summed else 2
+            nc.scalar.copy(out=turned_sb[q][:, :n, :], in_=turned[q][:, :n, :])
+            if q in summed:
+                store(*summed[q], q)
 
         def turn_back(q):
             back[q] = back_bank.tile([P, 2, TILE], F32, tag="back", name="back")
@@ -206,23 +217,29 @@ def tile_fast_tucker_taylor_pa_t_kernel(tc, z, G2, grad_out, out):
                     op=MULT,
                 )
 
-        def second_sum(g, i):
-            if g == LAST_GROUP:
-                sums[g, i] = vector_banks.tile([P, TILE], F32, tag="bank", name="last_sums")
-            else:
-                sums[g, i] = back_bank.tile([P, TILE], F32, tag="back", name="sums")
-            add_up(sums[g, i][:], prod[g, i])
+        summed = {}
 
-        def copy_result(g, i):
-            if i == 0:
-                result[g] = products.tile([P, 3, TILE], F32, name="result")
-            nc.scalar.copy(out=result[g][:, i, :], in_=sums[g, i][:])
+        def second_sum(g, i, q):
+            summed[q] = (g, i)
+            add_up(turned[q][:, 2, :], prod[g, i])
 
-        def store(g):
+        def last_sum(i):
+            sums[LAST_GROUP, i] = vector_banks.tile([P, TILE], F32, tag="bank", name="last_sums")
+            add_up(sums[LAST_GROUP, i][:], prod[LAST_GROUP, i])
+
+        def last_copy(i):
+            result[i] = products.tile([P, TILE], F32, name="result%d" % i)
+            nc.scalar.copy(out=result[i][:], in_=sums[LAST_GROUP, i][:])
+            store_tile(LAST_GROUP, i, result[i][:])
+
+        def store(g, i, q):
+            store_tile(g, i, turned_sb[q][:, 2, :])
+
+        def store_tile(g, i, source):
             for r in range(R):
                 nc.sync.dma_start(
-                    out=out[:, r, g * GROUP : (g + 1) * GROUP].rearrange("i (t m) -> t i m", m=TILE),
-                    in_=result[g][r:P:R, :, :],
+                    out=out[i, r, g * GROUP : (g + 1) * GROUP].rearrange("(t m) -> t m", m=TILE),
+                    in_=source[r:P:R, :],
                 )
 
         g2_raw = keep.tile([P, PACK, K], BF16)
@@ -256,61 +273,69 @@ def tile_fast_tucker_taylor_pa_t_kernel(tc, z, G2, grad_out, out):
                 out=z_t[:, :, i, :].rearrange("p (t g) r -> p g t r", g=R),
                 in_=z_bank[:].rearrange("p g (r t) -> p g t r", t=GROUP_TILES),
             )
-        quantise(0)
-        regroup_quad(1)
-        multiply(0, 0, vector_banks)
-        multiply(0, 1, vector_banks)
-        multiply(0, 2, scalar_banks)
-        regroup_quad(2)
-        quantise(1)
-
         def quad(q):
             return 0 <= q < N_QUADS
 
-        for q in range(N_QUADS + 2):
-            g, i = divmod(q - GROUP_QUADS - 3, GROUP_QUADS)
+        quantise(0)
+        regroup_quad(1)
+        multiply(0, 2, scalar_banks)
+        multiply(0, 0, vector_banks)
+        multiply(0, 1, vector_banks)
+        multiply(0, 3, scalar_banks)
+        quantise(1)
+        weigh(0, 0, 0)
+        weigh(0, 0, 1)
+        multiply(1, 2, scalar_banks)
+        seed(0)
+        weigh(0, 1, 0)
+        weigh(0, 1, 1)
+        regroup_quad(2)
+        quantise(2)
+        regroup_quad(3)
+
+        for q in range(0, N_QUADS + 2):
+            g, i = divmod(q - 6, GROUP_QUADS)
             summing = 0 <= g < LAST_GROUP and i < 3
-            if q % BLOCK_QUADS == 1 and 1 <= q // BLOCK_QUADS < N_BLOCKS - BLOCKS_IN_FLIGHT:
-                load(q // BLOCK_QUADS + BLOCKS_IN_FLIGHT)
-            if quad(q + 2):
-                quantise(q + 2)
-            if quad(q):
-                multiply(q, 3, scalar_banks, DOUBLED)
+            if q > 0 and (q) % BLOCK_QUADS == 0 and (q) // BLOCK_QUADS < N_BLOCKS - BLOCKS_IN_FLIGHT:
+                load((q) // BLOCK_QUADS + BLOCKS_IN_FLIGHT)
+            if quad(q + 3):
+                quantise(q + 3)
+            if quad(q + 1):
+                multiply(q + 1, 3, scalar_banks, 2)
             if quad(q + 1):
                 multiply(q + 1, 0, vector_banks)
-            if quad(q):
-                weigh(q, 0, 0)
-                weigh(q, 0, 1)
-            if quad(q - 2):
-                add_terms(q - 2, 1)
-            if summing:
-                second_sum(g, i)
             if quad(q + 1):
-                multiply(q + 1, 2, scalar_banks, DOUBLED)
-                multiply(q + 1, 1, vector_banks)
-            if quad(q):
-                weigh(q, 1, 0)
-            if quad(q - 2):
-                copy_turned(q - 2)
-            if summing:
-                copy_result(g, i)
-                if i == 2:
-                    store(g)
-            if quad(q):
-                weigh(q, 1, 1)
-            if quad(q - 2):
-                turn_back(q - 2)
+                weigh(q + 1, 0, 0)
+            if quad(q + 1):
+                weigh(q + 1, 0, 1)
             if quad(q - 1):
-                add_terms(q - 1, 0)
+                add_terms(q - 1, 1)
+            if summing:
+                second_sum(g, i, q - 1)
+            if quad(q + 1):
+                multiply(q + 1, 1, vector_banks)
+            if quad(q + 2):
+                multiply(q + 2, 2, scalar_banks, 2)
+            if quad(q + 1):
+                weigh(q + 1, 1, 0)
             if quad(q - 2):
                 copy_back(q - 2)
+            if quad(q - 2):
                 second_products(q - 2)
-            if quad(q + 3):
-                regroup_quad(q + 3)
+            if quad(q - 1):
+                copy_turned(q - 1)
+            if quad(q + 1):
+                weigh(q + 1, 1, 1)
+            if quad(q + 1):
+                seed(q + 1)
+            if quad(q - 1):
+                turn_back(q - 1)
+            if quad(q):
+                add_terms(q, 0)
+            if quad(q + 4):
+                regroup_quad(q + 4)
             if quad(q):
                 chains(q)
         for i in range(3):
-            second_sum(LAST_GROUP, i)
-        for i in range(3):
-            copy_result(LAST_GROUP, i)
-        store(LAST_GROUP)
+            last_sum(i)
+            last_copy(i)

@@ -33,7 +33,8 @@ BLOCK_QUADS = 4
 BLOCK = BLOCK_QUADS * LOAD
 N_BLOCKS = B // BLOCK
 BLOCKS_IN_FLIGHT = 3
-DOUBLED = 2
+SEED_T = lambda q: True
+SEED_U = lambda q: True
 
 FLOPS = 2 * Q * K * B
 
@@ -78,7 +79,7 @@ def tile_fast_tucker_taylor_pa_t_kernel(tc, z, G2, grad_out, out):
         g_rows = grad_out.rearrange("(p j) n -> p j n", j=PACK)
         g2_codes = keep.tile([P, K], U32, align_bytes=64)
         g2_scales = keep.tile([P, K], U8, align_bytes=64)
-        z_t = keep.tile([P, N_TILES, 3, R], F32)
+        z_t = [keep.tile([P, N_TILES, R], F32 if i != 1 else BF16, name="z_t%d" % i) for i in range(3)]
         ident = keep.tile([P, P], F32)
 
         raw, first_raw, grouped, codes, scales = {}, {}, {}, {}, {}
@@ -131,26 +132,27 @@ def tile_fast_tucker_taylor_pa_t_kernel(tc, z, G2, grad_out, out):
                 part[g] = partial.tile([P, 2, GROUP_TILES, RR], F32, name="part")
             return part[g], (q % GROUP_QUADS) * QUAD
 
-        def chains(q):
+        def sums_of(q):
             group_part, k = part_of(q)
-            for step in range(R - 1):
-                for s in range(2):
-                    tile_no = q * QUAD + s
-                    for which, take, factor in ((0, slice_c, 2), (1, slice_a, 0)):
-                        acc = group_part[:, which, k + s, :]
-                        weight = z_t[:, tile_no, factor, step : step + 1]
-                        accumulate(nc, acc, take(d_banks[q, s], step), weight, acc)
+            return [
+                (group_part[:, which, k + s, :], d_banks[q, s], take, z_t[factor][:, q * QUAD + s, :], seeded)
+                for which, take, factor, seeded in ((1, slice_a, 0, SEED_U), (0, slice_c, 2, SEED_T))
+                for s in range(2)
+            ]
+
+        def chains(q):
+            for step in range(R):
+                for acc, d_bank, take, weights, seeded in sums_of(q):
+                    weight = weights[:, step : step + 1]
+                    if step > 0:
+                        accumulate(nc, acc, take(d_bank, step), weight, acc)
+                    elif not seeded(q):
+                        nc.vector.tensor_scalar_mul(out=acc, in0=take(d_bank, step), scalar1=weight)
 
         def seed(q):
-            group_part, k = part_of(q)
-            last = R - 1
-            for s in range(2):
-                tile_no = q * QUAD + s
-                for which, take, factor in ((0, slice_c, 2), (1, slice_a, 0)):
-                    nc.scalar.activation(
-                        out=group_part[:, which, k + s, :], in_=take(d_banks[q, s], last), func=COPY,
-                        scale=z_t[:, tile_no, factor, last : last + 1],
-                    )
+            for acc, d_bank, take, weights, seeded in sums_of(q):
+                if seeded(q):
+                    nc.scalar.activation(out=acc, in_=take(d_bank, 0), func=COPY, scale=weights[:, 0:1])
 
         def weigh(q, s, which):
             if (s, which) == (0, 0):
@@ -163,7 +165,7 @@ def tile_fast_tucker_taylor_pa_t_kernel(tc, z, G2, grad_out, out):
             for step in range(R):
                 nc.scalar.activation(
                     out=terms[q][which][:, step, s, :], in_=take(d_banks[q, 2 + s], step), func=COPY,
-                    scale=z_t[:, tile_no, factor, step : step + 1],
+                    scale=z_t[factor][:, tile_no, step : step + 1],
                 )
 
         def add_up(bank_cols, slabs):
@@ -175,7 +177,10 @@ def tile_fast_tucker_taylor_pa_t_kernel(tc, z, G2, grad_out, out):
 
         def add_terms(q, which):
             if which == 0:
-                turned[q] = turn_bank.tile([P, 3, TILE], F32, tag="turn", name="turned")
+                if q == N_QUADS - 1:
+                    turned[q] = scalar_banks.tile([P, 3, TILE], F32, tag="bank", name="last_turned")
+                else:
+                    turned[q] = turn_bank.tile([P, 3, TILE], F32, tag="turn", name="turned")
             add_up(turned[q][:, which, :], terms[q][which])
 
         def copy_turned(q):
@@ -186,7 +191,10 @@ def tile_fast_tucker_taylor_pa_t_kernel(tc, z, G2, grad_out, out):
                 store(*summed[q], q)
 
         def turn_back(q):
-            back[q] = back_bank.tile([P, 2, TILE], F32, tag="back", name="back")
+            if q == N_QUADS - 1:
+                back[q] = scalar_banks.tile([P, 2, TILE], F32, tag="bank", name="last_back")
+            else:
+                back[q] = back_bank.tile([P, 2, TILE], F32, tag="back", name="back")
             for which in range(2):
                 nc.tensor.transpose(back[q][:, which, :], turned_sb[q][:, which, :], ident[:])
 
@@ -213,7 +221,7 @@ def tile_fast_tucker_taylor_pa_t_kernel(tc, z, G2, grad_out, out):
                 engine.tensor_tensor(
                     out=prod[g, i][:, :, k : k + QUAD, :].rearrange("p k t r -> p t k r"),
                     in0=first_sum,
-                    in1=z_t[:, tiles, factor, :].unsqueeze(3).to_broadcast([P, QUAD, R, R]),
+                    in1=z_t[factor][:, tiles, :].unsqueeze(3).to_broadcast([P, QUAD, R, R]),
                     op=MULT,
                 )
 
@@ -223,14 +231,14 @@ def tile_fast_tucker_taylor_pa_t_kernel(tc, z, G2, grad_out, out):
             summed[q] = (g, i)
             add_up(turned[q][:, 2, :], prod[g, i])
 
-        def last_sum(i):
-            sums[LAST_GROUP, i] = vector_banks.tile([P, TILE], F32, tag="bank", name="last_sums")
-            add_up(sums[LAST_GROUP, i][:], prod[LAST_GROUP, i])
+        def last_sum(g, i):
+            sums[g, i] = vector_banks.tile([P, TILE], F32, tag="bank", name="last_sums")
+            add_up(sums[g, i][:], prod[g, i])
 
-        def last_copy(i):
-            result[i] = products.tile([P, TILE], F32, name="result%d" % i)
-            nc.scalar.copy(out=result[i][:], in_=sums[LAST_GROUP, i][:])
-            store_tile(LAST_GROUP, i, result[i][:])
+        def last_copy(g, i):
+            result[g, i] = products.tile([P, TILE], F32, name="result%d" % i)
+            nc.scalar.copy(out=result[g, i][:], in_=sums[g, i][:])
+            store_tile(g, i, result[g, i][:])
 
         def store(g, i, q):
             store_tile(g, i, turned_sb[q][:, 2, :])
@@ -245,9 +253,17 @@ def tile_fast_tucker_taylor_pa_t_kernel(tc, z, G2, grad_out, out):
         g2_raw = keep.tile([P, PACK, K], BF16)
         nc.sync.dma_start(out=g2_raw[:], in_=G2.rearrange("(p j) k -> p j k", j=PACK))
         load_first(0)
-        z_rows = keep.tile([P, 3, B // GROUP_TILES], BF16)
-        nc.sync.dma_start(out=z_rows[:], in_=z.rearrange("i r (t x) -> (r t) i x", t=GROUP_TILES))
-        for q in range(1, BLOCK_QUADS):
+        z_rows = {}
+
+        def load_z(which):
+            for i in which:
+                z_rows[i] = keep.tile([P, B // GROUP_TILES], BF16, name="z_rows%d" % i)
+                nc.sync.dma_start(out=z_rows[i][:], in_=z[i].rearrange("r (t x) -> (r t) x", t=GROUP_TILES))
+
+        load_z((2, 0))
+        load_first(1)
+        load_z((1,))
+        for q in range(2, BLOCK_QUADS):
             load_first(q)
         for block in range(1, 1 + BLOCKS_IN_FLIGHT):
             load(block)
@@ -263,19 +279,26 @@ def tile_fast_tucker_taylor_pa_t_kernel(tc, z, G2, grad_out, out):
             scales=g2_scales[:],
             in_=g2_grouped[:].rearrange("p k j -> p (k j)"),
         )
-        for i in range(3):
-            z_bank = vector_banks.tile([P, R, TILE], BF16, tag="bank", name="z_bank")
-            for g in range(R):
-                nc.tensor.transpose(
-                    z_bank[:, g, :], z_rows[:, i, g * TILE : (g + 1) * TILE], ident_bf[:]
-                )
+        z_banks = {}
+
+        def turn_z(i, half):
+            pool, tag = ((turn_bank, "turn"), (back_bank, "back"))[half if i == 1 else i // 2]
+            z_banks[i, half] = pool.tile([P, R // 2, TILE], BF16, tag=tag, name="z_bank")
+            for g in range(R // 2):
+                first = (half * R // 2 + g) * TILE
+                nc.tensor.transpose(z_banks[i, half][:, g, :], z_rows[i][:, first : first + TILE], ident_bf[:])
+
+        def copy_z(i, half):
             nc.scalar.copy(
-                out=z_t[:, :, i, :].rearrange("p (t g) r -> p g t r", g=R),
-                in_=z_bank[:].rearrange("p g (r t) -> p g t r", t=GROUP_TILES),
+                out=z_t[i][:].rearrange("p (t h g) r -> p h g t r", h=2, g=R // 2)[:, half],
+                in_=z_banks[i, half][:].rearrange("p g (r t) -> p g t r", t=GROUP_TILES),
             )
+
         def quad(q):
             return 0 <= q < N_QUADS
 
+        turn_z(2, 0)
+        turn_z(0, 0)
         quantise(0)
         regroup_quad(1)
         multiply(0, 2, scalar_banks)
@@ -283,21 +306,34 @@ def tile_fast_tucker_taylor_pa_t_kernel(tc, z, G2, grad_out, out):
         multiply(0, 1, vector_banks)
         multiply(0, 3, scalar_banks)
         quantise(1)
+        copy_z(2, 0)
+        copy_z(0, 0)
         weigh(0, 0, 0)
         weigh(0, 0, 1)
-        multiply(1, 2, scalar_banks)
         seed(0)
+        turn_z(2, 1)
+        turn_z(0, 1)
+        multiply(1, 2, scalar_banks)
+        copy_z(2, 1)
+        copy_z(0, 1)
         weigh(0, 1, 0)
         weigh(0, 1, 1)
+        turn_z(1, 0)
+        turn_z(1, 1)
+        copy_z(1, 0)
+        copy_z(1, 1)
+        add_terms(0, 0)
         regroup_quad(2)
         quantise(2)
         regroup_quad(3)
 
-        for q in range(0, N_QUADS + 2):
-            g, i = divmod(q - 6, GROUP_QUADS)
-            summing = 0 <= g < LAST_GROUP and i < 3
+        for q in range(N_QUADS):
+            g, i = divmod(q - 5, GROUP_QUADS)
+            summing = 0 <= g < LAST_GROUP and i < 3 and q < N_QUADS - 1
             if q > 0 and (q) % BLOCK_QUADS == 0 and (q) // BLOCK_QUADS < N_BLOCKS - BLOCKS_IN_FLIGHT:
                 load((q) // BLOCK_QUADS + BLOCKS_IN_FLIGHT)
+            if quad(q):
+                chains(q)
             if quad(q + 3):
                 quantise(q + 3)
             if quad(q + 1):
@@ -308,34 +344,41 @@ def tile_fast_tucker_taylor_pa_t_kernel(tc, z, G2, grad_out, out):
                 weigh(q + 1, 0, 0)
             if quad(q + 1):
                 weigh(q + 1, 0, 1)
-            if quad(q - 1):
-                add_terms(q - 1, 1)
+            if q < N_QUADS - 1:
+                add_terms(q, 1)
             if summing:
-                second_sum(g, i, q - 1)
+                second_sum(g, i, q)
             if quad(q + 1):
                 multiply(q + 1, 1, vector_banks)
             if quad(q + 2):
                 multiply(q + 2, 2, scalar_banks, 2)
             if quad(q + 1):
                 weigh(q + 1, 1, 0)
-            if quad(q - 2):
-                copy_back(q - 2)
-            if quad(q - 2):
-                second_products(q - 2)
             if quad(q - 1):
-                copy_turned(q - 1)
+                copy_back(q - 1)
+            if quad(q - 1):
+                second_products(q - 1)
+            if quad(q):
+                copy_turned(q)
             if quad(q + 1):
                 weigh(q + 1, 1, 1)
             if quad(q + 1):
                 seed(q + 1)
-            if quad(q - 1):
-                turn_back(q - 1)
-            if quad(q):
-                add_terms(q, 0)
+            if q == N_QUADS - 2:
+                add_terms(q + 1, 0)
+                turn_back(q)
+                add_terms(q + 1, 1)
+            elif q < N_QUADS - 1:
+                turn_back(q)
+                add_terms(q + 1, 0)
+            else:
+                turn_back(q)
             if quad(q + 4):
                 regroup_quad(q + 4)
-            if quad(q):
-                chains(q)
+        copy_back(N_QUADS - 1)
+        second_products(N_QUADS - 1)
+        last_sum(LAST_GROUP - 1, 2)
+        last_copy(LAST_GROUP - 1, 2)
         for i in range(3):
-            last_sum(i)
-            last_copy(i)
+            last_sum(LAST_GROUP, i)
+            last_copy(LAST_GROUP, i)

@@ -337,7 +337,7 @@ def tile_fast_tucker_taylor_pa_t_kernel(tc, z, G2, grad_out, out):
             if quad(q + 3):
                 quantise(q + 3)
             if quad(q + 1):
-                multiply(q + 1, 3, scalar_banks, 2)
+                multiply(q + 1, 3, scalar_banks)
             if quad(q + 1):
                 multiply(q + 1, 0, vector_banks)
             if quad(q + 1):
@@ -351,7 +351,7 @@ def tile_fast_tucker_taylor_pa_t_kernel(tc, z, G2, grad_out, out):
             if quad(q + 1):
                 multiply(q + 1, 1, vector_banks)
             if quad(q + 2):
-                multiply(q + 2, 2, scalar_banks, 2)
+                multiply(q + 2, 2, scalar_banks)
             if quad(q + 1):
                 weigh(q + 1, 1, 0)
             if quad(q - 1):

@@ -33,8 +33,8 @@ BLOCK_QUADS = 4
 BLOCK = BLOCK_QUADS * LOAD
 N_BLOCKS = B // BLOCK
 BLOCKS_IN_FLIGHT = 3
-SEED_T = lambda q: True
-SEED_U = lambda q: True
+SEED_T = lambda q: 1 < q < N_QUADS - 1
+SEED_U = lambda q: 1 < q < N_QUADS - 1
 
 FLOPS = 2 * Q * K * B
 
@@ -169,32 +169,29 @@ def tile_fast_tucker_taylor_pa_t_kernel(tc, z, G2, grad_out, out):
                 )
 
         def add_up(bank_cols, slabs):
-            for step in range(R):
+            for step in reversed(range(R)):
                 nc.tensor.matmul(
                     out=bank_cols, lhsT=slabs[:, step].rearrange("p s x -> p (s x)"), rhs=ident[:],
-                    is_transpose=True, start=(step == 0), stop=(step == R - 1),
+                    is_transpose=True, start=(step == R - 1), stop=(step == 0),
                 )
 
         def add_terms(q, which):
             if which == 0:
                 if q == N_QUADS - 1:
-                    turned[q] = scalar_banks.tile([P, 3, TILE], F32, tag="bank", name="last_turned")
+                    turned[q] = scalar_banks.tile([P, 2, TILE], F32, tag="bank", name="last_turned")
                 else:
-                    turned[q] = turn_bank.tile([P, 3, TILE], F32, tag="turn", name="turned")
+                    turned[q] = turn_bank.tile([P, 2, TILE], F32, tag="turn", name="turned")
             add_up(turned[q][:, which, :], terms[q][which])
 
         def copy_turned(q):
-            turned_sb[q] = weighted.tile([P, 3, TILE], F32, name="turned_sb")
-            n = 3 if q in summed else 2
-            nc.scalar.copy(out=turned_sb[q][:, :n, :], in_=turned[q][:, :n, :])
-            if q in summed:
-                store(*summed[q], q)
+            turned_sb[q] = weighted.tile([P, 2, TILE], F32, name="turned_sb")
+            nc.scalar.copy(out=turned_sb[q][:], in_=turned[q][:])
 
         def turn_back(q):
             if q == N_QUADS - 1:
                 back[q] = scalar_banks.tile([P, 2, TILE], F32, tag="bank", name="last_back")
             else:
-                back[q] = back_bank.tile([P, 2, TILE], F32, tag="back", name="back")
+                back[q] = back_bank.tile([P, 3, TILE], F32, tag="back", name="back")
             for which in range(2):
                 nc.tensor.transpose(back[q][:, which, :], turned_sb[q][:, which, :], ident[:])
 
@@ -202,8 +199,13 @@ def tile_fast_tucker_taylor_pa_t_kernel(tc, z, G2, grad_out, out):
             group_part, k = part_of(q)
             nc.scalar.copy(
                 out=group_part[:, :, k + 2 : k + 4, :].rearrange("p w s x -> p w (s x)"),
-                in_=back[q][:],
+                in_=back[q][:, :2, :],
             )
+            if q in summed:
+                g, i = summed[q]
+                result[g, i] = products.tile([P, TILE], F32, name="result%d" % i)
+                nc.scalar.copy(out=result[g, i][:], in_=back[q][:, 2, :])
+                store_tile(g, i, result[g, i][:])
 
         def second_products(q):
             g, k = q // GROUP_QUADS, (q % GROUP_QUADS) * QUAD
@@ -229,7 +231,7 @@ def tile_fast_tucker_taylor_pa_t_kernel(tc, z, G2, grad_out, out):
 
         def second_sum(g, i, q):
             summed[q] = (g, i)
-            add_up(turned[q][:, 2, :], prod[g, i])
+            add_up(back[q][:, 2, :], prod[g, i])
 
         def last_sum(g, i):
             sums[g, i] = vector_banks.tile([P, TILE], F32, tag="bank", name="last_sums")
@@ -239,9 +241,6 @@ def tile_fast_tucker_taylor_pa_t_kernel(tc, z, G2, grad_out, out):
             result[g, i] = products.tile([P, TILE], F32, name="result%d" % i)
             nc.scalar.copy(out=result[g, i][:], in_=sums[g, i][:])
             store_tile(g, i, result[g, i][:])
-
-        def store(g, i, q):
-            store_tile(g, i, turned_sb[q][:, 2, :])
 
         def store_tile(g, i, source):
             for r in range(R):
@@ -346,8 +345,6 @@ def tile_fast_tucker_taylor_pa_t_kernel(tc, z, G2, grad_out, out):
                 weigh(q + 1, 0, 1)
             if q < N_QUADS - 1:
                 add_terms(q, 1)
-            if summing:
-                second_sum(g, i, q)
             if quad(q + 1):
                 multiply(q + 1, 1, vector_banks)
             if quad(q + 2):
@@ -368,9 +365,13 @@ def tile_fast_tucker_taylor_pa_t_kernel(tc, z, G2, grad_out, out):
                 add_terms(q + 1, 0)
                 turn_back(q)
                 add_terms(q + 1, 1)
+                if summing:
+                    second_sum(g, i, q)
             elif q < N_QUADS - 1:
                 turn_back(q)
                 add_terms(q + 1, 0)
+                if summing:
+                    second_sum(g, i, q)
             else:
                 turn_back(q)
             if quad(q + 4):

@@ -33,7 +33,7 @@ BLOCK_QUADS = 4
 BLOCK = BLOCK_QUADS * LOAD
 N_BLOCKS = B // BLOCK
 BLOCKS_IN_FLIGHT = 3
-SEED_T = lambda q: 1 < q < N_QUADS - 1
+SEED_T = lambda q: 1 < q < N_QUADS - 1 and q % 2 == 0
 SEED_U = lambda q: 1 < q < N_QUADS - 1
 
 FLOPS = 2 * Q * K * B
@@ -207,11 +207,12 @@ def tile_fast_tucker_taylor_pa_t_kernel(tc, z, G2, grad_out, out):
                 nc.scalar.copy(out=result[g, i][:], in_=back[q][:, 2, :])
                 store_tile(g, i, result[g, i][:])
 
-        def second_products(q):
-            g, k = q // GROUP_QUADS, (q % GROUP_QUADS) * QUAD
-            tiles = slice(q * QUAD, (q + 1) * QUAD)
-            t_part = part[g][:, 0, k : k + QUAD].rearrange("p t (b a) -> p t b a", a=R)
-            u_part = part[g][:, 1, k : k + QUAD].rearrange("p t (c b) -> p t c b", b=R)
+        def second_products(engine, q, first=0, stop=QUAD):
+            g = q // GROUP_QUADS
+            k, end = ((q % GROUP_QUADS) * QUAD + s for s in (first, stop))
+            tiles = slice(q * QUAD + first, q * QUAD + stop)
+            t_part = part[g][:, 0, k:end].rearrange("p t (b a) -> p t b a", a=R)
+            u_part = part[g][:, 1, k:end].rearrange("p t (c b) -> p t c b", b=R)
             for i, first_sum, factor in (
                 (0, t_part, 1),
                 (1, u_part, 2),
@@ -219,11 +220,10 @@ def tile_fast_tucker_taylor_pa_t_kernel(tc, z, G2, grad_out, out):
             ):
                 if k == 0:
                     prod[g, i] = products.tile([P, R, GROUP_TILES, R], F32, name="prod%d" % i)
-                engine = nc.vector if q == N_QUADS - 1 else nc.gpsimd
                 engine.tensor_tensor(
-                    out=prod[g, i][:, :, k : k + QUAD, :].rearrange("p k t r -> p t k r"),
+                    out=prod[g, i][:, :, k:end, :].rearrange("p k t r -> p t k r"),
                     in0=first_sum,
-                    in1=z_t[factor][:, tiles, :].unsqueeze(3).to_broadcast([P, QUAD, R, R]),
+                    in1=z_t[factor][:, tiles, :].unsqueeze(3).to_broadcast([P, stop - first, R, R]),
                     op=MULT,
                 )
 
@@ -281,7 +281,10 @@ def tile_fast_tucker_taylor_pa_t_kernel(tc, z, G2, grad_out, out):
         z_banks = {}
 
         def turn_z(i, half):
-            pool, tag = ((turn_bank, "turn"), (back_bank, "back"))[half if i == 1 else i // 2]
+            if half == 1 and i != 1:
+                pool, tag = vector_banks, "bank"
+            else:
+                pool, tag = (back_bank, "back") if half == 1 or i == 2 else (turn_bank, "turn")
             z_banks[i, half] = pool.tile([P, R // 2, TILE], BF16, tag=tag, name="z_bank")
             for g in range(R // 2):
                 first = (half * R // 2 + g) * TILE
@@ -298,27 +301,26 @@ def tile_fast_tucker_taylor_pa_t_kernel(tc, z, G2, grad_out, out):
 
         turn_z(2, 0)
         turn_z(0, 0)
+        copy_z(2, 0)
+        copy_z(0, 0)
         quantise(0)
         regroup_quad(1)
         multiply(0, 2, scalar_banks)
-        multiply(0, 0, vector_banks)
-        multiply(0, 1, vector_banks)
         multiply(0, 3, scalar_banks)
-        quantise(1)
-        copy_z(2, 0)
-        copy_z(0, 0)
-        weigh(0, 0, 0)
-        weigh(0, 0, 1)
-        seed(0)
         turn_z(2, 1)
         turn_z(0, 1)
-        multiply(1, 2, scalar_banks)
-        copy_z(2, 1)
-        copy_z(0, 1)
-        weigh(0, 1, 0)
-        weigh(0, 1, 1)
+        multiply(0, 0, vector_banks)
+        multiply(0, 1, vector_banks)
+        quantise(1)
+        weigh(0, 0, 0)
+        weigh(0, 0, 1)
         turn_z(1, 0)
         turn_z(1, 1)
+        multiply(1, 2, scalar_banks)
+        weigh(0, 1, 0)
+        weigh(0, 1, 1)
+        copy_z(2, 1)
+        copy_z(0, 1)
         copy_z(1, 0)
         copy_z(1, 1)
         add_terms(0, 0)
@@ -326,59 +328,62 @@ def tile_fast_tucker_taylor_pa_t_kernel(tc, z, G2, grad_out, out):
         quantise(2)
         regroup_quad(3)
 
-        for q in range(N_QUADS):
+        for q in range(N_QUADS - 2):
             g, i = divmod(q - 5, GROUP_QUADS)
-            summing = 0 <= g < LAST_GROUP and i < 3 and q < N_QUADS - 1
-            if q > 0 and (q) % BLOCK_QUADS == 0 and (q) // BLOCK_QUADS < N_BLOCKS - BLOCKS_IN_FLIGHT:
-                load((q) // BLOCK_QUADS + BLOCKS_IN_FLIGHT)
-            if quad(q):
-                chains(q)
+            summing = 0 <= g < LAST_GROUP and i < 3
+            if q > 0 and q % BLOCK_QUADS == 0 and q // BLOCK_QUADS < N_BLOCKS - BLOCKS_IN_FLIGHT:
+                load(q // BLOCK_QUADS + BLOCKS_IN_FLIGHT)
+            chains(q)
             if quad(q + 3):
                 quantise(q + 3)
-            if quad(q + 1):
-                multiply(q + 1, 3, scalar_banks)
-            if quad(q + 1):
-                multiply(q + 1, 0, vector_banks)
-            if quad(q + 1):
-                weigh(q + 1, 0, 0)
-            if quad(q + 1):
-                weigh(q + 1, 0, 1)
-            if q < N_QUADS - 1:
-                add_terms(q, 1)
-            if quad(q + 1):
-                multiply(q + 1, 1, vector_banks)
-            if quad(q + 2):
-                multiply(q + 2, 2, scalar_banks)
-            if quad(q + 1):
-                weigh(q + 1, 1, 0)
-            if quad(q - 1):
+            multiply(q + 1, 3, scalar_banks)
+            multiply(q + 1, 0, vector_banks)
+            weigh(q + 1, 0, 0)
+            weigh(q + 1, 0, 1)
+            add_terms(q, 1)
+            multiply(q + 1, 1, vector_banks)
+            multiply(q + 2, 2, scalar_banks)
+            weigh(q + 1, 1, 0)
+            if q > 0:
                 copy_back(q - 1)
-            if quad(q - 1):
-                second_products(q - 1)
-            if quad(q):
-                copy_turned(q)
-            if quad(q + 1):
-                weigh(q + 1, 1, 1)
-            if quad(q + 1):
-                seed(q + 1)
-            if q == N_QUADS - 2:
-                add_terms(q + 1, 0)
-                turn_back(q)
-                add_terms(q + 1, 1)
-                if summing:
-                    second_sum(g, i, q)
-            elif q < N_QUADS - 1:
-                turn_back(q)
-                add_terms(q + 1, 0)
-                if summing:
-                    second_sum(g, i, q)
-            else:
-                turn_back(q)
+                second_products(nc.gpsimd, q - 1)
+            copy_turned(q)
+            weigh(q + 1, 1, 1)
+            seed(q + 1)
+            turn_back(q)
+            add_terms(q + 1, 0)
+            if summing:
+                second_sum(g, i, q)
             if quad(q + 4):
                 regroup_quad(q + 4)
-        copy_back(N_QUADS - 1)
-        second_products(N_QUADS - 1)
+
+        q = N_QUADS - 2
+        chains(q)
+        multiply(q + 1, 3, scalar_banks)
+        multiply(q + 1, 0, vector_banks)
+        weigh(q + 1, 0, 0)
+        weigh(q + 1, 0, 1)
+        copy_back(q - 1)
+        second_products(nc.gpsimd, q - 1)
+        add_terms(q, 1)
+        multiply(q + 1, 1, vector_banks)
+        weigh(q + 1, 1, 0)
+        copy_turned(q)
+        add_terms(q + 1, 0)
+        turn_back(q)
+        weigh(q + 1, 1, 1)
+        copy_back(q)
+        add_terms(q + 1, 1)
+        chains(q + 1)
+        copy_turned(q + 1)
+        last_sum(LAST_GROUP - 1, 1)
+        turn_back(q + 1)
+        second_products(nc.vector, q)
+        second_products(nc.vector, q + 1, 0, 2)
+        copy_back(q + 1)
+        second_products(nc.vector, q + 1, 2, 4)
         last_sum(LAST_GROUP - 1, 2)
+        last_copy(LAST_GROUP - 1, 1)
         last_copy(LAST_GROUP - 1, 2)
         for i in range(3):
             last_sum(LAST_GROUP, i)

@@ -33,8 +33,8 @@ BLOCK_QUADS = 4
 BLOCK = BLOCK_QUADS * LOAD
 N_BLOCKS = B // BLOCK
 BLOCKS_IN_FLIGHT = 3
-SEED_T = lambda q: 1 < q < N_QUADS - 1 and q % 2 == 0
-SEED_U = lambda q: 1 < q < N_QUADS - 1
+SEED_T = lambda q: 2 <= q < 30
+SEED_U = lambda q: 2 <= q < 30
 
 FLOPS = 2 * Q * K * B
 

from contextlib import ExitStack

import concourse.mybir as mybir
from concourse.masks import make_identity

F32 = mybir.dt.float32
BF16 = mybir.dt.bfloat16
U32 = mybir.dt.uint32
U8 = mybir.dt.uint8
E4M3_X4 = mybir.dt.float8_e4m3fn_x4
E5M2_X4 = mybir.dt.float8_e5m2_x4
MULT = mybir.AluOpType.mult
ADD = mybir.AluOpType.add
COPY = mybir.ActivationFunctionType.Copy

P = 128
PACK = 4
Q = P * PACK
R = 8
RR = R * R
K = R * R * R
B = 16384
TILE = P
N_TILES = B // TILE
GROUP_TILES = P // R
GROUP = GROUP_TILES * TILE
QUAD = 4
LOAD = QUAD * TILE
N_QUADS = B // LOAD
GROUP_QUADS = GROUP_TILES // QUAD
LAST_GROUP = N_QUADS // GROUP_QUADS - 1
BLOCK_QUADS = 4
BLOCK = BLOCK_QUADS * LOAD
N_BLOCKS = B // BLOCK
BLOCKS_IN_FLIGHT = 3
SEED_T = lambda q: 2 <= q < 30
SEED_U = lambda q: 2 <= q < 30

FLOPS = 2 * Q * K * B


def regroup(copy, grouped, raw):
    copy(
        out=grouped.rearrange("p (c i) j -> p c j i", i=4),
        in_=raw.rearrange("p j (c i) -> p c j i", i=4),
    )


def slice_c(d_bank, c):
    return d_bank[:, c * RR : (c + 1) * RR]


def slice_a(d_bank, a):
    return d_bank[:].rearrange("p (cb a) -> p cb a", a=R)[:, :, a]


def accumulate(nc, acc, d_slice, weight, so_far):
    nc.vector.scalar_tensor_tensor(
        out=acc, in0=d_slice, scalar=weight, in1=so_far, op0=MULT, op1=ADD
    )


def tile_fast_tucker_taylor_pa_t_kernel(tc, z, G2, grad_out, out):
    nc = tc.nc
    with ExitStack() as ctx:
        keep = ctx.enter_context(tc.tile_pool(name="keep", bufs=1))
        loads = ctx.enter_context(tc.tile_pool(name="loads", bufs=BLOCKS_IN_FLIGHT))
        stage = ctx.enter_context(tc.tile_pool(name="stage", bufs=2))
        operand = ctx.enter_context(tc.tile_pool(name="operand", bufs=5))
        partial = ctx.enter_context(tc.tile_pool(name="partial", bufs=3))
        weighted = ctx.enter_context(tc.tile_pool(name="weighted", bufs=3))
        products = ctx.enter_context(tc.tile_pool(name="products", bufs=2))
        vector_banks = ctx.enter_context(tc.psum_pool(name="vector_banks", bufs=4))
        scalar_banks = ctx.enter_context(tc.psum_pool(name="scalar_banks", bufs=2))
        turn_bank = ctx.enter_context(tc.psum_pool(name="turn_bank", bufs=1))
        back_bank = ctx.enter_context(tc.psum_pool(name="back_bank", bufs=1))
        ctx.enter_context(tc.manual_schedule())

        g_rows = grad_out.rearrange("(p j) n -> p j n", j=PACK)
        g2_codes = keep.tile([P, K], U32, align_bytes=64)
        g2_scales = keep.tile([P, K], U8, align_bytes=64)
        z_t = [keep.tile([P, N_TILES, R], F32 if i != 1 else BF16, name="z_t%d" % i) for i in range(3)]
        ident = keep.tile([P, P], F32)

        raw, first_raw, grouped, codes, scales = {}, {}, {}, {}, {}
        d_banks, terms, turned, turned_sb, back = {}, {}, {}, {}, {}
        part, prod, sums, result = {}, {}, {}, {}

        def load(block):
            raw[block] = loads.tile([P, PACK, BLOCK], BF16, name="raw")
            nc.sync.dma_start(out=raw[block][:], in_=g_rows[:, :, block * BLOCK : (block + 1) * BLOCK])

        def load_first(q):
            first_raw[q] = keep.tile([P, PACK, LOAD], BF16, name="first_raw%d" % q)
            nc.sync.dma_start(out=first_raw[q][:], in_=g_rows[:, :, q * LOAD : (q + 1) * LOAD])

        def regroup_quad(q):
            grouped[q] = stage.tile([P, LOAD, PACK], BF16, align_bytes=64, name="grouped")
            block, place = divmod(q, BLOCK_QUADS)
            if block == 0:
                source = first_raw[q][:]
            else:
                source = raw[block][:, :, place * LOAD : (place + 1) * LOAD]
            regroup(nc.vector.tensor_copy, grouped[q][:], source)

        def quantise(q):
            codes[q] = operand.tile([P, LOAD], U32, align_bytes=64, name="codes")
            scales[q] = operand.tile([P, LOAD], U8, align_bytes=64, name="scales")
            nc.vector.quantize_mx(
                out=codes[q][:].bitcast(E5M2_X4),
                scales=scales[q][:],
                in_=grouped[q][:].rearrange("p w j -> p (w j)"),
            )

        def multiply(q, s, pool, times=1):
            cols = slice(s * TILE, (s + 1) * TILE)
            d_banks[q, s] = pool.tile([P, K], F32, tag="bank", name="d_bank")
            for again in range(times):
                nc.tensor.matmul_mx(
                    out=d_banks[q, s][:],
                    lhsT=codes[q][:, cols].bitcast(E5M2_X4),
                    lhsT_scale=scales[q][:, cols],
                    rhs=g2_codes[:].bitcast(E4M3_X4),
                    rhs_scale=g2_scales[:],
                    start=True,
                    stop=True,
                )

        def part_of(q):
            g = q // GROUP_QUADS
            if g not in part:
                part[g] = partial.tile([P, 2, GROUP_TILES, RR], F32, name="part")
            return part[g], (q % GROUP_QUADS) * QUAD

        def sums_of(q):
            group_part, k = part_of(q)
            return [
                (group_part[:, which, k + s, :], d_banks[q, s], take, z_t[factor][:, q * QUAD + s, :], seeded)
                for which, take, factor, seeded in ((1, slice_a, 0, SEED_U), (0, slice_c, 2, SEED_T))
                for s in range(2)
            ]

        def chains(q):
            for step in range(R):
                for acc, d_bank, take, weights, seeded in sums_of(q):
                    weight = weights[:, step : step + 1]
                    if step > 0:
                        accumulate(nc, acc, take(d_bank, step), weight, acc)
                    elif not seeded(q):
                        nc.vector.tensor_scalar_mul(out=acc, in0=take(d_bank, step), scalar1=weight)

        def seed(q):
            for acc, d_bank, take, weights, seeded in sums_of(q):
                if seeded(q):
                    nc.scalar.activation(out=acc, in_=take(d_bank, 0), func=COPY, scale=weights[:, 0:1])

        def weigh(q, s, which):
            if (s, which) == (0, 0):
                terms[q] = (
                    weighted.tile([P, R, 2, RR], F32, name="t_terms"),
                    weighted.tile([P, R, 2, RR], F32, name="u_terms"),
                )
            tile_no = q * QUAD + 2 + s
            take, factor = ((slice_c, 2), (slice_a, 0))[which]
            for step in range(R):
                nc.scalar.activation(
                    out=terms[q][which][:, step, s, :], in_=take(d_banks[q, 2 + s], step), func=COPY,
                    scale=z_t[factor][:, tile_no, step : step + 1],
                )

        def add_up(bank_cols, slabs):
            for step in reversed(range(R)):
                nc.tensor.matmul(
                    out=bank_cols, lhsT=slabs[:, step].rearrange("p s x -> p (s x)"), rhs=ident[:],
                    is_transpose=True, start=(step == R - 1), stop=(step == 0),
                )

        def add_terms(q, which):
            if which == 0:
                if q == N_QUADS - 1:
                    turned[q] = scalar_banks.tile([P, 2, TILE], F32, tag="bank", name="last_turned")
                else:
                    turned[q] = turn_bank.tile([P, 2, TILE], F32, tag="turn", name="turned")
            add_up(turned[q][:, which, :], terms[q][which])

        def copy_turned(q):
            turned_sb[q] = weighted.tile([P, 2, TILE], F32, name="turned_sb")
            nc.scalar.copy(out=turned_sb[q][:], in_=turned[q][:])

        def turn_back(q):
            if q == N_QUADS - 1:
                back[q] = scalar_banks.tile([P, 2, TILE], F32, tag="bank", name="last_back")
            else:
                back[q] = back_bank.tile([P, 3, TILE], F32, tag="back", name="back")
            for which in range(2):
                nc.tensor.transpose(back[q][:, which, :], turned_sb[q][:, which, :], ident[:])

        def copy_back(q):
            group_part, k = part_of(q)
            nc.scalar.copy(
                out=group_part[:, :, k + 2 : k + 4, :].rearrange("p w s x -> p w (s x)"),
                in_=back[q][:, :2, :],
            )
            if q in summed:
                g, i = summed[q]
                result[g, i] = products.tile([P, TILE], F32, name="result%d" % i)
                nc.scalar.copy(out=result[g, i][:], in_=back[q][:, 2, :])
                store_tile(g, i, result[g, i][:])

        def second_products(engine, q, first=0, stop=QUAD):
            g = q // GROUP_QUADS
            k, end = ((q % GROUP_QUADS) * QUAD + s for s in (first, stop))
            tiles = slice(q * QUAD + first, q * QUAD + stop)
            t_part = part[g][:, 0, k:end].rearrange("p t (b a) -> p t b a", a=R)
            u_part = part[g][:, 1, k:end].rearrange("p t (c b) -> p t c b", b=R)
            for i, first_sum, factor in (
                (0, t_part, 1),
                (1, u_part, 2),
                (2, u_part.rearrange("p t c b -> p t b c"), 1),
            ):
                if k == 0:
                    prod[g, i] = products.tile([P, R, GROUP_TILES, R], F32, name="prod%d" % i)
                engine.tensor_tensor(
                    out=prod[g, i][:, :, k:end, :].rearrange("p k t r -> p t k r"),
                    in0=first_sum,
                    in1=z_t[factor][:, tiles, :].unsqueeze(3).to_broadcast([P, stop - first, R, R]),
                    op=MULT,
                )

        summed = {}

        def second_sum(g, i, q):
            summed[q] = (g, i)
            add_up(back[q][:, 2, :], prod[g, i])

        def last_sum(g, i):
            sums[g, i] = vector_banks.tile([P, TILE], F32, tag="bank", name="last_sums")
            add_up(sums[g, i][:], prod[g, i])

        def last_copy(g, i):
            result[g, i] = products.tile([P, TILE], F32, name="result%d" % i)
            nc.scalar.copy(out=result[g, i][:], in_=sums[g, i][:])
            store_tile(g, i, result[g, i][:])

        def store_tile(g, i, source):
            for r in range(R):
                nc.sync.dma_start(
                    out=out[i, r, g * GROUP : (g + 1) * GROUP].rearrange("(t m) -> t m", m=TILE),
                    in_=source[r:P:R, :],
                )

        g2_raw = keep.tile([P, PACK, K], BF16)
        nc.sync.dma_start(out=g2_raw[:], in_=G2.rearrange("(p j) k -> p j k", j=PACK))
        load_first(0)
        z_rows = {}

        def load_z(which):
            for i in which:
                z_rows[i] = keep.tile([P, B // GROUP_TILES], BF16, name="z_rows%d" % i)
                nc.sync.dma_start(out=z_rows[i][:], in_=z[i].rearrange("r (t x) -> (r t) x", t=GROUP_TILES))

        load_z((2, 0))
        load_first(1)
        load_z((1,))
        for q in range(2, BLOCK_QUADS):
            load_first(q)
        for block in range(1, 1 + BLOCKS_IN_FLIGHT):
            load(block)
        ident_bf = keep.tile([P, P], BF16)
        make_identity(nc, ident_bf[:])
        make_identity(nc, ident[:])

        g2_grouped = keep.tile([P, K, PACK], BF16, align_bytes=64)
        regroup(nc.vector.tensor_copy, g2_grouped[:], g2_raw[:])
        regroup_quad(0)
        nc.vector.quantize_mx(
            out=g2_codes[:].bitcast(E4M3_X4),
            scales=g2_scales[:],
            in_=g2_grouped[:].rearrange("p k j -> p (k j)"),
        )
        z_banks = {}

        def turn_z(i, half):
            if half == 1 and i != 1:
                pool, tag = vector_banks, "bank"
            else:
                pool, tag = (back_bank, "back") if half == 1 or i == 2 else (turn_bank, "turn")
            z_banks[i, half] = pool.tile([P, R // 2, TILE], BF16, tag=tag, name="z_bank")
            for g in range(R // 2):
                first = (half * R // 2 + g) * TILE
                nc.tensor.transpose(z_banks[i, half][:, g, :], z_rows[i][:, first : first + TILE], ident_bf[:])

        def copy_z(i, half):
            nc.scalar.copy(
                out=z_t[i][:].rearrange("p (t h g) r -> p h g t r", h=2, g=R // 2)[:, half],
                in_=z_banks[i, half][:].rearrange("p g (r t) -> p g t r", t=GROUP_TILES),
            )

        def quad(q):
            return 0 <= q < N_QUADS

        turn_z(2, 0)
        turn_z(0, 0)
        copy_z(2, 0)
        copy_z(0, 0)
        quantise(0)
        regroup_quad(1)
        multiply(0, 2, scalar_banks)
        multiply(0, 3, scalar_banks)
        turn_z(2, 1)
        turn_z(0, 1)
        multiply(0, 0, vector_banks)
        multiply(0, 1, vector_banks)
        quantise(1)
        weigh(0, 0, 0)
        weigh(0, 0, 1)
        turn_z(1, 0)
        turn_z(1, 1)
        multiply(1, 2, scalar_banks)
        weigh(0, 1, 0)
        weigh(0, 1, 1)
        copy_z(2, 1)
        copy_z(0, 1)
        copy_z(1, 0)
        copy_z(1, 1)
        add_terms(0, 0)
        regroup_quad(2)
        quantise(2)
        regroup_quad(3)

        for q in range(N_QUADS - 2):
            g, i = divmod(q - 5, GROUP_QUADS)
            summing = 0 <= g < LAST_GROUP and i < 3
            if q > 0 and q % BLOCK_QUADS == 0 and q // BLOCK_QUADS < N_BLOCKS - BLOCKS_IN_FLIGHT:
                load(q // BLOCK_QUADS + BLOCKS_IN_FLIGHT)
            chains(q)
            if quad(q + 3):
                quantise(q + 3)
            multiply(q + 1, 3, scalar_banks)
            multiply(q + 1, 0, vector_banks)
            weigh(q + 1, 0, 0)
            weigh(q + 1, 0, 1)
            add_terms(q, 1)
            multiply(q + 1, 1, vector_banks)
            multiply(q + 2, 2, scalar_banks)
            weigh(q + 1, 1, 0)
            if q > 0:
                copy_back(q - 1)
                second_products(nc.gpsimd, q - 1)
            copy_turned(q)
            weigh(q + 1, 1, 1)
            seed(q + 1)
            turn_back(q)
            add_terms(q + 1, 0)
            if summing:
                second_sum(g, i, q)
            if quad(q + 4):
                regroup_quad(q + 4)

        q = N_QUADS - 2
        chains(q)
        multiply(q + 1, 3, scalar_banks)
        multiply(q + 1, 0, vector_banks)
        weigh(q + 1, 0, 0)
        weigh(q + 1, 0, 1)
        copy_back(q - 1)
        second_products(nc.gpsimd, q - 1)
        add_terms(q, 1)
        multiply(q + 1, 1, vector_banks)
        weigh(q + 1, 1, 0)
        copy_turned(q)
        add_terms(q + 1, 0)
        turn_back(q)
        weigh(q + 1, 1, 1)
        copy_back(q)
        add_terms(q + 1, 1)
        chains(q + 1)
        copy_turned(q + 1)
        last_sum(LAST_GROUP - 1, 1)
        turn_back(q + 1)
        second_products(nc.vector, q)
        second_products(nc.vector, q + 1, 0, 2)
        copy_back(q + 1)
        second_products(nc.vector, q + 1, 2, 4)
        last_sum(LAST_GROUP - 1, 2)
        last_copy(LAST_GROUP - 1, 1)
        last_copy(LAST_GROUP - 1, 2)
        for i in range(3):
            last_sum(LAST_GROUP, i)
            last_copy(LAST_GROUP, i)
